import numpy as np
import ml_dtypes


def mxq(x, axis, fmt="e4m3"):
    dtype, down = {"e4m3": (ml_dtypes.float8_e4m3fn, 7), "e5m2": (ml_dtypes.float8_e5m2, 14)}[fmt]
    v = np.moveaxis(np.asarray(x, np.float32).astype(ml_dtypes.bfloat16).astype(np.float64), axis, -1)
    blocks = v.reshape(v.shape[:-1] + (-1, 32))
    amax = np.abs(blocks).max(-1, keepdims=True)
    byte = np.maximum(np.where(amax > 0, np.frexp(amax)[1] - 1 + 127, 0) - down, 1)
    scale = np.exp2(byte - 127.0)
    codes = (blocks / scale).astype(np.float32).astype(dtype).astype(np.float64)
    return np.moveaxis((codes * scale).reshape(v.shape), -1, axis)


WIDE = False


def mx_kscale(k):
    if not WIDE:
        return np.ones(k)
    levels = np.array([10, -10, 5, -5, 0])
    a = np.random.permutation(np.resize(levels, k // 512 * 4)).reshape(k // 512, 4)
    idx = np.arange(k)
    return np.exp2(a[idx // 512, idx % 128 // 32])


BF16 = ml_dtypes.bfloat16


def bf(x):
    return np.asarray(x, np.float32).astype(BF16)


def f64(x):
    return np.asarray(x).astype(np.float64)


E2M1 = np.array([0.0, 0.5, 1.0, 1.5, 2.0, 3.0, 4.0, 6.0, -0.0, -0.5, -1.0, -1.5, -2.0, -3.0, -4.0, -6.0])


def pack_weight(w, fmt):
    k, n = w.shape
    w = f64(bf(w)).reshape(k // 32, 32, n)
    amax = np.abs(w).max(1)
    if fmt == "e4m3":
        byte = np.frexp(amax)[1] - 1 + 127 - 7
    else:
        mant, ex = np.frexp(amax / 6.0)
        byte = np.where(mant > 0.5, ex, ex - 1) + 127
    byte = np.clip(np.where(amax > 0, byte, 1), 1, 254)
    scaled = (w * np.exp2(127.0 - byte)[:, None, :]).reshape(k, n).astype(np.float32)
    by_word = np.ascontiguousarray(scaled.reshape(k // 512, 128, 4, n).transpose(0, 1, 3, 2))
    if fmt == "e4m3":
        words = by_word.astype(ml_dtypes.float8_e4m3fn).view(np.uint8)
    else:
        c = by_word.astype(ml_dtypes.float4_e2m1fn).view(np.uint8) & 0xF
        words = c[..., 0::2] | (c[..., 1::2] << 4)
    return np.ascontiguousarray(words), np.ascontiguousarray(byte.astype(np.uint8).reshape(k // 512, 16, n))


def unpack_weight(words, scales, fmt):
    g, p, n, _ = words.shape
    if fmt == "e4m3":
        vals = np.ascontiguousarray(words).view(ml_dtypes.float8_e4m3fn).astype(np.float64)
    else:
        nib = np.empty((g, p, n, 4), np.uint8)
        nib[..., 0::2] = words & 0xF
        nib[..., 1::2] = words >> 4
        vals = E2M1[nib]
    vals = vals * np.repeat(np.exp2(scales.astype(np.float64) - 127.0), 8, axis=1)[..., None]
    return vals.transpose(0, 1, 3, 2).reshape(g * 512, n)

def pack4(w):
    words, scales = pack_weight(w, "e2m1")
    return words.reshape(words.shape[0], 128, -1), scales


def unpack4(words, scales):
    return unpack_weight(words.reshape(words.shape[0], 128, -1, 2), scales, "e2m1")


B, S, D, O, G, P = 2, 512, 512, 512, 3, 3
NB = G + P


def silu(v):
    return v / (1.0 + np.exp(-v))


def extended_grid(d):
    pts = np.linspace(-1.0, 1.0, G + 1)
    h = 2.0 / G
    left = pts[0] + h * np.arange(-P, 0)
    right = pts[-1] + h * np.arange(1, P + 1)
    ext = np.concatenate([left, pts, right])
    return np.broadcast_to(ext, (d, ext.shape[0]))


def bspline_basis(x, grid):
    x = x[:, :, None]
    g = grid[None, :, :]
    bb = ((x >= g[..., :-1]) & (x < g[..., 1:])).astype(np.float64)
    for p in range(1, P + 1):
        left = (x - g[..., :-(p + 1)]) / (g[..., p:-1] - g[..., :-(p + 1)])
        right = (g[..., p + 1:] - x) / (g[..., p + 1:] - g[..., 1:-p])
        bb = left * bb[..., :-1] + right * bb[..., 1:]
    return bb


def setup_inputs():
    s = mx_kscale(D)
    u = s / s.max()
    x = bf(np.random.standard_normal((B, S, D)) * u)
    coef = bf(np.random.standard_normal((O, D, NB)) * 2.0 / np.sqrt(D))
    scale_base = (0.25 + (np.random.uniform(size=(O, D)) * 2.0 - 1.0) * 2.0) / np.sqrt(D) / u
    words, scales = pack4(np.ascontiguousarray(scale_base.T))
    scale_sp = bf(1.0 + 0.1 * np.random.standard_normal((O, D)))
    bias = bf(0.1 * np.random.standard_normal(O))
    return {"x": x,
            "coef": coef,
            "scale_base_words": words,
            "scale_base_scales": scales,
            "scale_sp": scale_sp,
            "bias": bias}


def reference(x, coef, scale_base_words, scale_base_scales, scale_sp, bias):
    x = f64(x)
    b_, s_, d = x.shape
    xf = x.reshape(-1, d)
    grid = extended_grid(d)
    basis = bspline_basis(xf, grid)
    base = silu(xf)
    spline_w = f64(scale_sp)[..., None] * f64(coef)
    y_base = mxq(base, 1, "e4m3") @ unpack4(scale_base_words, scale_base_scales)
    bt = np.ascontiguousarray(basis.transpose(2, 0, 1))
    wt = np.ascontiguousarray(spline_w.transpose(2, 1, 0))
    y_sp = (mxq(bt, 2, "e4m3") @ mxq(wt, 1, "e4m3")).sum(0)
    y = y_base + y_sp + f64(bias)[None, :]
    return y.reshape(b_, s_, -1)

@@ -1,0 +1,256 @@
+import math
+from contextlib import ExitStack
+
+import concourse.mybir as mybir
+from concourse.masks import make_identity
+
+F32 = mybir.dt.float32
+BF16 = mybir.dt.bfloat16
+U8 = mybir.dt.uint8
+U32 = mybir.dt.uint32
+I32 = mybir.dt.int32
+FP8X4 = mybir.dt.float8_e4m3fn_x4
+FP4X4 = mybir.dt.float4_e2m1fn_x4
+ALU = mybir.AluOpType
+ACT = mybir.ActivationFunctionType
+
+P = 128
+N_ROWS = 1024
+D = 512
+O = 512
+NB = 6
+FLOPS = 2 * N_ROWS * D * O * (NB + 1)
+
+TILES = N_ROWS // P
+CH_T = 2
+CHUNKS = TILES // CH_T
+C = CH_T * P * 4
+ACT_COEF = (0, 1, 2)
+SLOTS = (-1, 2, 3, 0, 4, 1, 5)
+
+
+def tile_kanoriginal_kernel(tc, x, coef, scale_base_words, scale_base_scales, scale_sp, bias, out):
+    nc = tc.nc
+    k6 = math.sqrt(1.0 / 6.0)
+    k2 = math.sqrt(0.5)
+    with ExitStack() as ctx:
+        const = ctx.enter_context(tc.tile_pool(name="const", bufs=1))
+        cpool = ctx.enter_context(tc.tile_pool(name="cpool", bufs=2))
+        xgp = ctx.enter_context(tc.tile_pool(name="xgp", bufs=2))
+        fp = ctx.enter_context(tc.tile_pool(name="fp", bufs=2))
+        hp = ctx.enter_context(tc.tile_pool(name="hp", bufs=2))
+        actp = ctx.enter_context(tc.tile_pool(name="actp", bufs=2))
+        qp = ctx.enter_context(tc.tile_pool(name="qp", bufs=3))
+        op = ctx.enter_context(tc.tile_pool(name="op", bufs=2))
+        pst = ctx.enter_context(tc.psum_pool(name="pst", bufs=3))
+        pso = ctx.enter_context(tc.psum_pool(name="pso", bufs=4))
+
+        w4s = const.tile([P, O], U8, align_bytes=64)
+        nc.vector.memset(w4s[:].bitcast(I32), 0)
+        ident = const.tile([P, P], F32)
+        make_identity(nc, ident[:])
+
+        xv = x.flatten_outer_dims().rearrange("(p j) d -> p j d", j=TILES)
+        ov = out.flatten_outer_dims().rearrange("(p j) o -> p j o", j=TILES)
+        cv = coef.rearrange("(a o) i b -> a o (i b)", o=P)
+        x_sb = const.tile([P, TILES, D], BF16)
+        sp_sb = const.tile([P, 4, D], BF16)
+        w4 = const.tile([P, 2 * O], U8, align_bytes=64)
+        bias_sb = const.tile([P, O], BF16)
+        coef_sb = []
+
+        def load_coef(a):
+            ct = cpool.tile([P, D * NB], BF16, tag="coef", name="coef%d" % a)
+            nc.sync.dma_start(out=ct[:], in_=cv[a])
+            coef_sb.append(ct)
+
+        nc.sync.dma_start(out=x_sb[:, 0:2, :], in_=xv[:, 0:2, :])
+        for q in range(4):
+            nc.sync.dma_start(
+                out=w4s[32 * q : 32 * q + 4, :].bitcast(I32),
+                in_=scale_base_scales[0, 4 * q : 4 * q + 4, :].bitcast(I32),
+            )
+        nc.sync.dma_start(out=sp_sb[:], in_=scale_sp.rearrange("(a o) i -> o a i", o=P))
+        load_coef(0)
+        nc.sync.dma_start(out=x_sb[:, 2:8, :], in_=xv[:, 2:8, :])
+        load_coef(1)
+        nc.sync.dma_start(out=w4[:].bitcast(I32), in_=scale_base_words[0].bitcast(I32))
+        nc.scalar.dma_start(out=bias_sb[:], in_=bias.partition_broadcast(P))
+
+        def transpose_x(c):
+            xt = pst.tile([P, 512], F32, tag="tp", name="xt%d" % c)
+            xtv = xt[:].rearrange("p (j u n) -> p j u n", j=CH_T, u=2)
+            for jj in range(CH_T):
+                words = x_sb[:, c * CH_T + jj, :].bitcast(F32)
+                for u in range(2):
+                    nc.tensor.transpose(xtv[:, jj, u, :], words[:, u : D // 2 : 2], ident[:])
+            xg = xgp.tile([P, CH_T, P, 4], BF16, align_bytes=64, tag="xg", name="xg%d" % c)
+            nc.scalar.copy(out=xg[:].bitcast(F32), in_=xtv.rearrange("p j u n -> p j n u"))
+            return xg
+
+        spg = const.tile([P, O, 4], BF16)
+        wg = const.tile([P, NB, O, 4], BF16, align_bytes=64)
+        wc = const.tile([P, NB, O], U32, align_bytes=64)
+        ws = const.tile([P, NB, O], U8, align_bytes=64)
+
+        def transpose_sp():
+            for h in range(2):
+                st = pst.tile([P, 512], F32, tag="tp", name="st%d" % h)
+                stv = st[:].rearrange("p (a u o) -> p a u o", a=2, u=2)
+                for aa in range(2):
+                    words = sp_sb[:, 2 * h + aa, :].bitcast(F32)
+                    for u in range(2):
+                        nc.tensor.transpose(stv[:, aa, u, :], words[:, u : D // 2 : 2], ident[:])
+                nc.scalar.copy(
+                    out=spg[:, 256 * h : 256 * (h + 1), :].bitcast(F32).rearrange("p (a o) u -> p a o u", a=2),
+                    in_=stv.rearrange("p a u o -> p a o u"),
+                )
+
+        def weights(a):
+            cwords = coef_sb[a][:].bitcast(F32)
+            cols = slice(a * P, (a + 1) * P)
+            for beta in range(3):
+                wt = pst.tile([P, 512], F32, tag="tp", name="wt%d_%d" % (a, beta))
+                for t in range(4):
+                    nc.tensor.transpose(
+                        wt[:, t * P : (t + 1) * P], cwords[:, 3 * t + beta : D * 3 : 12], ident[:]
+                    )
+                src = wt[:].bitcast(BF16).rearrange("p (t o e) -> p e o t", t=4, e=2)
+                dst = wg[:, 2 * beta : 2 * beta + 2, cols, :]
+                if a in ACT_COEF:
+                    nc.scalar.copy(out=dst, in_=src)
+                else:
+                    nc.vector.tensor_tensor(
+                        out=dst, in0=src, in1=spg[:, cols, :].unsqueeze(1).to_broadcast([P, 2, P, 4]), op=ALU.mult
+                    )
+            if a in ACT_COEF:
+                whole = wg[:, :, cols, :].rearrange("p b o t -> p b (o t)")
+                nc.vector.tensor_tensor(
+                    out=whole,
+                    in0=whole,
+                    in1=spg[:, cols, :].rearrange("p o t -> p (o t)").unsqueeze(1).to_broadcast([P, NB, 4 * P]),
+                    op=ALU.mult,
+                )
+
+        def quantise_weights():
+            for b in range(NB):
+                nc.vector.quantize_mx(
+                    out=wc[:, b, :].bitcast(FP8X4),
+                    scales=ws[:, b, :],
+                    in_=wg[:, b, :, :].rearrange("p o t -> p (o t)"),
+                )
+
+        own_tag = ("v1e", "v1o", "v2e", "v2o", "nfo", "nfe", "m4", "m5")
+
+        def ftile(nm):
+            if nm in own_tag:
+                return fp.tile([P, C], F32, tag=nm, name=nm)
+            return fp.tile([P, C], F32, tag="f", name=nm, bufs=7)
+
+        def htile(nm):
+            if nm in own_tag:
+                return hp.tile([P, C], BF16, tag=nm, name=nm)
+            return hp.tile([P, C], BF16, tag="h", name=nm, bufs=6)
+
+        def act_fn(nm, src, func, scale, bias_, half=False):
+            t = htile(nm) if half else ftile(nm)
+            nc.scalar.activation(out=t[:], in_=src, func=func, scale=scale, bias=bias_)
+            return t
+
+        codes = {}
+
+        def elementwise(c, xg):
+            xf = xg[:].rearrange("p j n t -> p (j n t)")
+            act = actp.tile([P, NB + 1, C], BF16, align_bytes=64, tag="act", name="act%d" % c)
+            ac = qp.tile([P, NB + 1, C // 4], U32, align_bytes=64, tag="ac", name="ac%d" % c)
+            asc = qp.tile([P, NB + 1, C // 4], U8, align_bytes=64, tag="asc", name="asc%d" % c)
+            codes[c] = (ac, asc)
+
+            def quantise(s0, s1):
+                nc.vector.quantize_mx(
+                    out=ac[:, s0:s1, :].rearrange("p g w -> p (g w)").bitcast(FP8X4),
+                    scales=asc[:, s0:s1, :].rearrange("p g w -> p (g w)"),
+                    in_=act[:, s0:s1, :].rearrange("p g w -> p (g w)"),
+                )
+
+            v1e = act_fn("v1e", xf, ACT.Abs, 1.5, 0.5)
+            v2e = act_fn("v2e", v1e[:], ACT.Abs, 1.0, -2.0)
+            g = act_fn("g", v2e[:], ACT.Abs, 1.0, -1.0)
+            sqg = act_fn("sqg", g[:], ACT.Square, k2, 0.0)
+            sqe = act_fn("sqe", g[:], ACT.Square, -k2, k2)
+            eo = ftile("eo")
+            nc.vector.scalar_tensor_tensor(out=eo[:], in0=g[:], scalar=2.0, in1=sqg[:], op0=ALU.subtract, op1=ALU.mult)
+            ee = ftile("ee")
+            nc.vector.scalar_tensor_tensor(out=ee[:], in0=g[:], scalar=1.0, in1=sqe[:], op0=ALU.add, op1=ALU.mult)
+            v1o = act_fn("v1o", xf, ACT.Abs, 1.5, -0.5)
+            v2o = act_fn("v2o", v1o[:], ACT.Abs, 1.0, -2.0)
+            nfo = act_fn("nfo", eo[:], ACT.Identity, -1.0, -2.0 / 3.0, half=True)
+            nfe = act_fn("nfe", ee[:], ACT.Identity, 1.0, -2.0 / 3.0, half=True)
+            m4 = htile("m4")
+            nc.vector.tensor_scalar(out=m4[:], in0=xf, scalar1=-1.0 / 3.0, scalar2=None, op0=ALU.is_lt)
+            m5 = htile("m5")
+            nc.vector.tensor_scalar(out=m5[:], in0=xf, scalar1=1.0 / 3.0, scalar2=None, op0=ALU.is_lt)
+
+            def spline(nm, a, nf, dst):
+                s = act_fn("s" + nm, a[:], ACT.Square, k6, -2.0 * k6)
+                nw = htile("nw" + nm)
+                nc.vector.scalar_tensor_tensor(out=nw[:], in0=a[:], scalar=2.0, in1=s[:], op0=ALU.subtract, op1=ALU.mult)
+                tm = htile("tm" + nm)
+                nc.vector.tensor_tensor(out=tm[:], in0=nw[:], in1=nf[:], op=ALU.max)
+                nc.vector.tensor_scalar(out=dst, in0=tm[:], scalar1=0.0, scalar2=-1.0, op0=ALU.min, op1=ALU.mult)
+
+            nc.scalar.activation(out=act[:, 0, :], in_=xf, func=ACT.Silu)
+            spline("2", v1e, nfe, act[:, 1, :])
+            spline("3", v1o, nfo, act[:, 2, :])
+            quantise(0, 1)
+            ya = htile("ya")
+            spline("A", v2e, nfe, ya[:])
+            nc.vector.tensor_tensor(out=act[:, 3, :], in0=ya[:], in1=m4[:], op=ALU.mult)
+            nc.vector.tensor_tensor(out=act[:, 4, :], in0=ya[:], in1=act[:, 3, :], op=ALU.subtract)
+            quantise(1, 3)
+            yb = htile("yb")
+            spline("B", v2o, nfo, yb[:])
+            nc.vector.tensor_tensor(out=act[:, 5, :], in0=yb[:], in1=m5[:], op=ALU.mult)
+            nc.vector.tensor_tensor(out=act[:, 6, :], in0=yb[:], in1=act[:, 5, :], op=ALU.subtract)
+            quantise(3, 5)
+            quantise(5, 7)
+
+        def matmuls(c):
+            ac, asc = codes[c]
+            res = op.tile([P, CH_T, O], F32, tag="res", name="res%d" % c)
+            for jj in range(CH_T):
+                acc = pso.tile([P, O], F32, tag="acc", name="acc%d_%d" % (c, jj))
+                cols = slice(jj * P, (jj + 1) * P)
+                for s, b in enumerate(SLOTS):
+                    nc.tensor.matmul_mx(
+                        out=acc[:],
+                        lhsT=ac[:, s, cols].bitcast(FP8X4),
+                        lhsT_scale=asc[:, s, cols],
+                        rhs=(w4[:].bitcast(FP4X4) if b < 0 else wc[:, b, :].bitcast(FP8X4)),
+                        rhs_scale=(w4s[:] if b < 0 else ws[:, b, :]),
+                        start=(s == 0),
+                        stop=(s == NB),
+                    )
+                nc.vector.tensor_tensor(out=res[:, jj, :], in0=acc[:], in1=bias_sb[:], op=ALU.add)
+            nc.sync.dma_start(out=ov[:, c * CH_T : (c + 1) * CH_T, :], in_=res[:])
+
+        xg0 = transpose_x(0)
+        xg1 = transpose_x(1)
+        elementwise(0, xg0)
+        transpose_sp()
+        weights(0)
+        load_coef(2)
+        weights(1)
+        load_coef(3)
+        xg2 = transpose_x(2)
+        elementwise(1, xg1)
+        weights(2)
+        weights(3)
+        quantise_weights()
+        matmuls(0)
+        matmuls(1)
+        xg3 = transpose_x(3)
+        elementwise(2, xg2)
+        matmuls(2)
+        elementwise(3, xg3)
+        matmuls(3)

@@ -25,30 +25,39 @@ TILES = N_ROWS // P
 CH_T = 2
 CHUNKS = TILES // CH_T
 C = CH_T * P * 4
-ACT_COEF = (0, 1, 2)
-SLOTS = (-1, 2, 3, 0, 4, 1, 5)
+DVE_COEF = (0,)
+MANUAL = True
+N_SLOTS = 9
+PASSES = ((1, 2), (2, 0), (3, 4), (4, -1), (6, 3), (7, 1), (8, 5))
 
 
 def tile_kanoriginal_kernel(tc, x, coef, scale_base_words, scale_base_scales, scale_sp, bias, out):
     nc = tc.nc
     k6 = math.sqrt(1.0 / 6.0)
     k2 = math.sqrt(0.5)
+    r0 = (2.0 - 2.0 ** (2.0 / 3.0) - 2.0 ** (4.0 / 3.0)) / 3.0
+    beta = r0 - 2.0
+    dl = (r0 * beta - beta * beta / 4.0) / 2.0
     with ExitStack() as ctx:
         const = ctx.enter_context(tc.tile_pool(name="const", bufs=1))
-        cpool = ctx.enter_context(tc.tile_pool(name="cpool", bufs=2))
-        xgp = ctx.enter_context(tc.tile_pool(name="xgp", bufs=2))
-        fp = ctx.enter_context(tc.tile_pool(name="fp", bufs=2))
+        cpool = ctx.enter_context(tc.tile_pool(name="cpool", bufs=3))
+        fp = ctx.enter_context(tc.tile_pool(name="fp", bufs=1))
         hp = ctx.enter_context(tc.tile_pool(name="hp", bufs=2))
         actp = ctx.enter_context(tc.tile_pool(name="actp", bufs=2))
-        qp = ctx.enter_context(tc.tile_pool(name="qp", bufs=3))
+        qp = ctx.enter_context(tc.tile_pool(name="qp", bufs=2))
         op = ctx.enter_context(tc.tile_pool(name="op", bufs=2))
-        pst = ctx.enter_context(tc.psum_pool(name="pst", bufs=3))
+        pst = ctx.enter_context(tc.psum_pool(name="pst", bufs=4))
         pso = ctx.enter_context(tc.psum_pool(name="pso", bufs=4))
+        if MANUAL:
+            ctx.enter_context(tc.manual_schedule())
 
         w4s = const.tile([P, O], U8, align_bytes=64)
         nc.vector.memset(w4s[:].bitcast(I32), 0)
+        warm = const.tile([P, 8], F32)
+        nc.vector.memset(warm[:], 0.0)
         ident = const.tile([P, P], F32)
         make_identity(nc, ident[:])
+        nc.scalar.activation(out=warm[:, 4:8], in_=warm[:, 0:4], func=ACT.Silu)
 
         xv = x.flatten_outer_dims().rearrange("(p j) d -> p j d", j=TILES)
         ov = out.flatten_outer_dims().rearrange("(p j) o -> p j o", j=TILES)
@@ -65,17 +74,22 @@ def tile_kanoriginal_kernel(tc, x, coef, scale_base_words, scale_base_scales, sc
             coef_sb.append(ct)
 
         nc.sync.dma_start(out=x_sb[:, 0:2, :], in_=xv[:, 0:2, :])
+        nc.sync.dma_start(out=sp_sb[:], in_=scale_sp.rearrange("(a o) i -> o a i", o=P))
+        load_coef(0)
+        nc.sync.dma_start(out=x_sb[:, 2:8, :], in_=xv[:, 2:8, :])
+        load_coef(1)
+        load_coef(2)
+        load_coef(3)
         for q in range(4):
             nc.sync.dma_start(
                 out=w4s[32 * q : 32 * q + 4, :].bitcast(I32),
                 in_=scale_base_scales[0, 4 * q : 4 * q + 4, :].bitcast(I32),
             )
-        nc.sync.dma_start(out=sp_sb[:], in_=scale_sp.rearrange("(a o) i -> o a i", o=P))
-        load_coef(0)
-        nc.sync.dma_start(out=x_sb[:, 2:8, :], in_=xv[:, 2:8, :])
-        load_coef(1)
         nc.sync.dma_start(out=w4[:].bitcast(I32), in_=scale_base_words[0].bitcast(I32))
         nc.scalar.dma_start(out=bias_sb[:], in_=bias.partition_broadcast(P))
+
+        xg = const.tile([P, TILES, P, 4], BF16, align_bytes=64)
+        below = const.tile([P, 2, TILES * P * 4], BF16)
 
         def transpose_x(c):
             xt = pst.tile([P, 512], F32, tag="tp", name="xt%d" % c)
@@ -84,9 +98,9 @@ def tile_kanoriginal_kernel(tc, x, coef, scale_base_words, scale_base_scales, sc
                 words = x_sb[:, c * CH_T + jj, :].bitcast(F32)
                 for u in range(2):
                     nc.tensor.transpose(xtv[:, jj, u, :], words[:, u : D // 2 : 2], ident[:])
-            xg = xgp.tile([P, CH_T, P, 4], BF16, align_bytes=64, tag="xg", name="xg%d" % c)
-            nc.scalar.copy(out=xg[:].bitcast(F32), in_=xtv.rearrange("p j u n -> p j n u"))
-            return xg
+            nc.vector.tensor_copy(
+                out=xg[:, c * CH_T : (c + 1) * CH_T, :, :].bitcast(F32), in_=xtv.rearrange("p j u n -> p j n u")
+            )
 
         spg = const.tile([P, O, 4], BF16)
         wg = const.tile([P, NB, O, 4], BF16, align_bytes=64)
@@ -101,7 +115,7 @@ def tile_kanoriginal_kernel(tc, x, coef, scale_base_words, scale_base_scales, sc
                     words = sp_sb[:, 2 * h + aa, :].bitcast(F32)
                     for u in range(2):
                         nc.tensor.transpose(stv[:, aa, u, :], words[:, u : D // 2 : 2], ident[:])
-                nc.scalar.copy(
+                nc.vector.tensor_copy(
                     out=spg[:, 256 * h : 256 * (h + 1), :].bitcast(F32).rearrange("p (a o) u -> p a o u", a=2),
                     in_=stv.rearrange("p a u o -> p a o u"),
                 )
@@ -109,21 +123,19 @@ def tile_kanoriginal_kernel(tc, x, coef, scale_base_words, scale_base_scales, sc
         def weights(a):
             cwords = coef_sb[a][:].bitcast(F32)
             cols = slice(a * P, (a + 1) * P)
-            for beta in range(3):
-                wt = pst.tile([P, 512], F32, tag="tp", name="wt%d_%d" % (a, beta))
+            for bp in range(3):
+                wt = pst.tile([P, 512], F32, tag="tp", name="wt%d_%d" % (a, bp))
                 for t in range(4):
-                    nc.tensor.transpose(
-                        wt[:, t * P : (t + 1) * P], cwords[:, 3 * t + beta : D * 3 : 12], ident[:]
-                    )
+                    nc.tensor.transpose(wt[:, t * P : (t + 1) * P], cwords[:, 3 * t + bp : D * 3 : 12], ident[:])
                 src = wt[:].bitcast(BF16).rearrange("p (t o e) -> p e o t", t=4, e=2)
-                dst = wg[:, 2 * beta : 2 * beta + 2, cols, :]
-                if a in ACT_COEF:
-                    nc.scalar.copy(out=dst, in_=src)
-                else:
+                dst = wg[:, 2 * bp : 2 * bp + 2, cols, :]
+                if a in DVE_COEF:
                     nc.vector.tensor_tensor(
                         out=dst, in0=src, in1=spg[:, cols, :].unsqueeze(1).to_broadcast([P, 2, P, 4]), op=ALU.mult
                     )
-            if a in ACT_COEF:
+                else:
+                    nc.scalar.copy(out=dst, in_=src)
+            if a not in DVE_COEF:
                 whole = wg[:, :, cols, :].rearrange("p b o t -> p b (o t)")
                 nc.vector.tensor_tensor(
                     out=whole,
@@ -133,37 +145,35 @@ def tile_kanoriginal_kernel(tc, x, coef, scale_base_words, scale_base_scales, sc
                 )
 
         def quantise_weights():
-            for b in range(NB):
+            for b in range(0, NB, 2):
                 nc.vector.quantize_mx(
-                    out=wc[:, b, :].bitcast(FP8X4),
-                    scales=ws[:, b, :],
-                    in_=wg[:, b, :, :].rearrange("p o t -> p (o t)"),
+                    out=wc[:, b : b + 2, :].rearrange("p b o -> p (b o)").bitcast(FP8X4),
+                    scales=ws[:, b : b + 2, :].rearrange("p b o -> p (b o)"),
+                    in_=wg[:, b : b + 2, :, :].rearrange("p b o t -> p (b o t)"),
                 )
 
-        own_tag = ("v1e", "v1o", "v2e", "v2o", "nfo", "nfe", "m4", "m5")
+        def afn(dst, src, func, scale, shift):
+            nc.scalar.activation(out=dst, in_=src, func=func, scale=scale, bias=shift)
 
-        def ftile(nm):
-            if nm in own_tag:
-                return fp.tile([P, C], F32, tag=nm, name=nm)
-            return fp.tile([P, C], F32, tag="f", name=nm, bufs=7)
-
-        def htile(nm):
-            if nm in own_tag:
-                return hp.tile([P, C], BF16, tag=nm, name=nm)
-            return hp.tile([P, C], BF16, tag="h", name=nm, bufs=6)
-
-        def act_fn(nm, src, func, scale, bias_, half=False):
-            t = htile(nm) if half else ftile(nm)
-            nc.scalar.activation(out=t[:], in_=src, func=func, scale=scale, bias=bias_)
-            return t
+        def tt(dst, in0, in1, op_):
+            nc.vector.tensor_tensor(out=dst, in0=in0, in1=in1, op=op_)
 
         codes = {}
+        accs = {}
 
-        def elementwise(c, xg):
-            xf = xg[:].rearrange("p j n t -> p (j n t)")
-            act = actp.tile([P, NB + 1, C], BF16, align_bytes=64, tag="act", name="act%d" % c)
-            ac = qp.tile([P, NB + 1, C // 4], U32, align_bytes=64, tag="ac", name="ac%d" % c)
-            asc = qp.tile([P, NB + 1, C // 4], U8, align_bytes=64, tag="asc", name="asc%d" % c)
+        def evacuate(c, jj):
+            if jj == 0:
+                accs[(c, "res")] = op.tile([P, CH_T, O], F32, tag="res", name="res%d" % c)
+            res = accs[(c, "res")]
+            tt(res[:, jj, :], accs[(c, jj)][:], bias_sb[:], ALU.add)
+            if jj == CH_T - 1:
+                nc.sync.dma_start(out=ov[:, c * CH_T : (c + 1) * CH_T, :], in_=res[:])
+
+        def elementwise(c, prev):
+            xf = xg[:, c * CH_T : (c + 1) * CH_T, :, :].rearrange("p j n t -> p (j n t)")
+            act = actp.tile([P, N_SLOTS, C], BF16, align_bytes=64, tag="act", name="act%d" % c)
+            ac = qp.tile([P, N_SLOTS, C // 4], U32, align_bytes=64, tag="ac", name="ac%d" % c)
+            asc = qp.tile([P, N_SLOTS, C // 4], U8, align_bytes=64, tag="asc", name="asc%d" % c)
             codes[c] = (ac, asc)
 
             def quantise(s0, s1):
@@ -173,84 +183,90 @@ def tile_kanoriginal_kernel(tc, x, coef, scale_base_words, scale_base_scales, sc
                     in_=act[:, s0:s1, :].rearrange("p g w -> p (g w)"),
                 )
 
-            v1e = act_fn("v1e", xf, ACT.Abs, 1.5, 0.5)
-            v2e = act_fn("v2e", v1e[:], ACT.Abs, 1.0, -2.0)
-            g = act_fn("g", v2e[:], ACT.Abs, 1.0, -1.0)
-            sqg = act_fn("sqg", g[:], ACT.Square, k2, 0.0)
-            sqe = act_fn("sqe", g[:], ACT.Square, -k2, k2)
-            eo = ftile("eo")
-            nc.vector.scalar_tensor_tensor(out=eo[:], in0=g[:], scalar=2.0, in1=sqg[:], op0=ALU.subtract, op1=ALU.mult)
-            ee = ftile("ee")
-            nc.vector.scalar_tensor_tensor(out=ee[:], in0=g[:], scalar=1.0, in1=sqe[:], op0=ALU.add, op1=ALU.mult)
-            v1o = act_fn("v1o", xf, ACT.Abs, 1.5, -0.5)
-            v2o = act_fn("v2o", v1o[:], ACT.Abs, 1.0, -2.0)
-            nfo = act_fn("nfo", eo[:], ACT.Identity, -1.0, -2.0 / 3.0, half=True)
-            nfe = act_fn("nfe", ee[:], ACT.Identity, 1.0, -2.0 / 3.0, half=True)
-            m4 = htile("m4")
-            nc.vector.tensor_scalar(out=m4[:], in0=xf, scalar1=-1.0 / 3.0, scalar2=None, op0=ALU.is_lt)
-            m5 = htile("m5")
-            nc.vector.tensor_scalar(out=m5[:], in0=xf, scalar1=1.0 / 3.0, scalar2=None, op0=ALU.is_lt)
+            afn(act[:, 4, :], xf, ACT.Silu, 1.0, 0.0)
+            tiles = {}
+            for par, shift1 in (("e", 0.5), ("o", -0.5)):
+                v = fp.tile([P, 2, C], F32, tag="v" + par, name="v" + par)
+                afn(v[:, 1, :], xf, ACT.Abs, 1.5, shift1)
+                afn(v[:, 0, :], v[:, 1, :], ACT.Abs, 1.0, -2.0)
+                if par == "e":
+                    g = fp.tile([P, C], F32, tag="g", name="g")
+                    afn(g[:], v[:, 0, :], ACT.Abs, 1.0, -1.0)
+                sq = fp.tile([P, C], F32, tag="sq" + par, name="sq" + par)
+                h = fp.tile([P, C], F32, tag="h" + par, name="h" + par)
+                if par == "e":
+                    afn(sq[:], g[:], ACT.Square, -k2, k2 * (1.0 + beta / 2.0))
+                    afn(h[:], g[:], ACT.Identity, 1.0, r0 - 1.0)
+                else:
+                    afn(sq[:], g[:], ACT.Square, k2, k2 * beta / 2.0)
+                    afn(h[:], g[:], ACT.Identity, -1.0, r0)
+                s = fp.tile([P, 2, C], F32, tag="s" + par, name="s" + par)
+                afn(s[:], v[:], ACT.Square, k6, -2.0 * k6)
+                tiles[par] = (v, sq, h, s)
 
-            def spline(nm, a, nf, dst):
-                s = act_fn("s" + nm, a[:], ACT.Square, k6, -2.0 * k6)
-                nw = htile("nw" + nm)
-                nc.vector.scalar_tensor_tensor(out=nw[:], in0=a[:], scalar=2.0, in1=s[:], op0=ALU.subtract, op1=ALU.mult)
-                tm = htile("tm" + nm)
-                nc.vector.tensor_tensor(out=tm[:], in0=nw[:], in1=nf[:], op=ALU.max)
-                nc.vector.tensor_scalar(out=dst, in0=tm[:], scalar1=0.0, scalar2=-1.0, op0=ALU.min, op1=ALU.mult)
-
-            nc.scalar.activation(out=act[:, 0, :], in_=xf, func=ACT.Silu)
-            spline("2", v1e, nfe, act[:, 1, :])
-            spline("3", v1o, nfo, act[:, 2, :])
-            quantise(0, 1)
-            ya = htile("ya")
-            spline("A", v2e, nfe, ya[:])
-            nc.vector.tensor_tensor(out=act[:, 3, :], in0=ya[:], in1=m4[:], op=ALU.mult)
-            nc.vector.tensor_tensor(out=act[:, 4, :], in0=ya[:], in1=act[:, 3, :], op=ALU.subtract)
-            quantise(1, 3)
-            yb = htile("yb")
-            spline("B", v2o, nfo, yb[:])
-            nc.vector.tensor_tensor(out=act[:, 5, :], in0=yb[:], in1=m5[:], op=ALU.mult)
-            nc.vector.tensor_tensor(out=act[:, 6, :], in0=yb[:], in1=act[:, 5, :], op=ALU.subtract)
-            quantise(3, 5)
-            quantise(5, 7)
+            for par, base, mi in (("e", 0, 0), ("o", 5, 1)):
+                v, sq, h, s = tiles[par]
+                nf = hp.tile([P, C], BF16, tag="nf", name="nf" + par)
+                nc.vector.scalar_tensor_tensor(out=nf[:], in0=sq[:], scalar=dl, in1=h[:], op0=ALU.add, op1=ALU.mult)
+                nw = hp.tile([P, 2, C], BF16, tag="nw", name="nw" + par)
+                nc.vector.scalar_tensor_tensor(
+                    out=nw[:].rearrange("p r w -> p (r w)"),
+                    in0=v[:].rearrange("p r w -> p (r w)"),
+                    scalar=2.0,
+                    in1=s[:].rearrange("p r w -> p (r w)"),
+                    op0=ALU.subtract,
+                    op1=ALU.mult,
+                )
+                if prev is not None:
+                    evacuate(prev, mi)
+                tt(nw[:], nw[:], nf[:].unsqueeze(1).to_broadcast([P, 2, C]), ALU.max)
+                if par == "o":
+                    quantise(1, 5)
+                nc.vector.tensor_scalar(
+                    out=act[:, base : base + 2, :], in0=nw[:], scalar1=0.0, scalar2=-1.0, op0=ALU.min, op1=ALU.mult
+                )
+                mk = below[:, mi, c * C : (c + 1) * C]
+                tt(act[:, base + 2, :], act[:, base, :], mk, ALU.mult)
+                tt(act[:, base + 3, :], act[:, base, :], act[:, base + 2, :], ALU.subtract)
+            quantise(6, 7)
+            quantise(7, 9)
 
         def matmuls(c):
             ac, asc = codes[c]
-            res = op.tile([P, CH_T, O], F32, tag="res", name="res%d" % c)
             for jj in range(CH_T):
                 acc = pso.tile([P, O], F32, tag="acc", name="acc%d_%d" % (c, jj))
+                accs[(c, jj)] = acc
                 cols = slice(jj * P, (jj + 1) * P)
-                for s, b in enumerate(SLOTS):
+                for n, (s, b) in enumerate(PASSES):
                     nc.tensor.matmul_mx(
                         out=acc[:],
                         lhsT=ac[:, s, cols].bitcast(FP8X4),
                         lhsT_scale=asc[:, s, cols],
                         rhs=(w4[:].bitcast(FP4X4) if b < 0 else wc[:, b, :].bitcast(FP8X4)),
                         rhs_scale=(w4s[:] if b < 0 else ws[:, b, :]),
-                        start=(s == 0),
-                        stop=(s == NB),
+                        start=(n == 0),
+                        stop=(n == NB),
                     )
-                nc.vector.tensor_tensor(out=res[:, jj, :], in0=acc[:], in1=bias_sb[:], op=ALU.add)
-            nc.sync.dma_start(out=ov[:, c * CH_T : (c + 1) * CH_T, :], in_=res[:])
 
-        xg0 = transpose_x(0)
-        xg1 = transpose_x(1)
-        elementwise(0, xg0)
+        transpose_x(0)
         transpose_sp()
         weights(0)
-        load_coef(2)
+        for c in range(1, CHUNKS):
+            transpose_x(c)
+        xall = xg[:].rearrange("p j n t -> p (j n t)")
+        nc.vector.tensor_scalar(out=below[:, 0, :], in0=xall, scalar1=-1.0 / 3.0, scalar2=None, op0=ALU.is_lt)
+        nc.vector.tensor_scalar(out=below[:, 1, :], in0=xall, scalar1=1.0 / 3.0, scalar2=None, op0=ALU.is_lt)
+        elementwise(0, None)
         weights(1)
-        load_coef(3)
-        xg2 = transpose_x(2)
-        elementwise(1, xg1)
         weights(2)
         weights(3)
         quantise_weights()
         matmuls(0)
+        elementwise(1, 0)
         matmuls(1)
-        xg3 = transpose_x(3)
-        elementwise(2, xg2)
+        elementwise(2, 1)
         matmuls(2)
-        elementwise(3, xg3)
+        elementwise(3, 2)
         matmuls(3)
+        evacuate(3, 0)
+        evacuate(3, 1)

@@ -28,7 +28,7 @@ C = CH_T * P * 4
 DVE_COEF = (0,)
 MANUAL = True
 N_SLOTS = 9
-PASSES = ((1, 2), (2, 0), (3, 4), (4, -1), (6, 3), (7, 1), (8, 5))
+PASSES = ((8, -1), (2, 2), (3, 3), (4, 0), (5, 1), (6, 4), (7, 5))
 
 
 def tile_kanoriginal_kernel(tc, x, coef, scale_base_words, scale_base_scales, scale_sp, bias, out):
@@ -40,9 +40,9 @@ def tile_kanoriginal_kernel(tc, x, coef, scale_base_words, scale_base_scales, sc
     dl = (r0 * beta - beta * beta / 4.0) / 2.0
     with ExitStack() as ctx:
         const = ctx.enter_context(tc.tile_pool(name="const", bufs=1))
-        cpool = ctx.enter_context(tc.tile_pool(name="cpool", bufs=3))
+        cpool = ctx.enter_context(tc.tile_pool(name="cpool", bufs=2))
         fp = ctx.enter_context(tc.tile_pool(name="fp", bufs=1))
-        hp = ctx.enter_context(tc.tile_pool(name="hp", bufs=2))
+        hp = ctx.enter_context(tc.tile_pool(name="hp", bufs=1))
         actp = ctx.enter_context(tc.tile_pool(name="actp", bufs=2))
         qp = ctx.enter_context(tc.tile_pool(name="qp", bufs=2))
         op = ctx.enter_context(tc.tile_pool(name="op", bufs=2))
@@ -152,8 +152,13 @@ def tile_kanoriginal_kernel(tc, x, coef, scale_base_words, scale_base_scales, sc
                     in_=wg[:, b : b + 2, :, :].rearrange("p b o t -> p (b o t)"),
                 )
 
-        def afn(dst, src, func, scale, shift):
-            nc.scalar.activation(out=dst, in_=src, func=func, scale=scale, bias=shift)
+        def afn(nm, src, func, scale, shift):
+            t = fp.tile([P, C], F32, tag=nm, name=nm)
+            nc.scalar.activation(out=t[:], in_=src, func=func, scale=scale, bias=shift)
+            return t
+
+        def stt(dst, in0, scalar, in1, op0):
+            nc.vector.scalar_tensor_tensor(out=dst, in0=in0, scalar=scalar, in1=in1, op0=op0, op1=ALU.mult)
 
         def tt(dst, in0, in1, op_):
             nc.vector.tensor_tensor(out=dst, in0=in0, in1=in1, op=op_)
@@ -172,67 +177,63 @@ def tile_kanoriginal_kernel(tc, x, coef, scale_base_words, scale_base_scales, sc
         def elementwise(c, prev):
             xf = xg[:, c * CH_T : (c + 1) * CH_T, :, :].rearrange("p j n t -> p (j n t)")
             act = actp.tile([P, N_SLOTS, C], BF16, align_bytes=64, tag="act", name="act%d" % c)
-            ac = qp.tile([P, N_SLOTS, C // 4], U32, align_bytes=64, tag="ac", name="ac%d" % c)
-            asc = qp.tile([P, N_SLOTS, C // 4], U8, align_bytes=64, tag="asc", name="asc%d" % c)
-            codes[c] = (ac, asc)
+            ac = qp.tile([P, N_SLOTS - 2, C // 4], U32, align_bytes=64, tag="ac", name="ac%d" % c)
+            asc = qp.tile([P, N_SLOTS - 2, C // 4], U8, align_bytes=64, tag="asc", name="asc%d" % c)
+            codes[c] = (ac, asc, act)
 
             def quantise(s0, s1):
                 nc.vector.quantize_mx(
-                    out=ac[:, s0:s1, :].rearrange("p g w -> p (g w)").bitcast(FP8X4),
-                    scales=asc[:, s0:s1, :].rearrange("p g w -> p (g w)"),
+                    out=ac[:, s0 - 2 : s1 - 2, :].rearrange("p g w -> p (g w)").bitcast(FP8X4),
+                    scales=asc[:, s0 - 2 : s1 - 2, :].rearrange("p g w -> p (g w)"),
                     in_=act[:, s0:s1, :].rearrange("p g w -> p (g w)"),
                 )
 
-            afn(act[:, 4, :], xf, ACT.Silu, 1.0, 0.0)
-            tiles = {}
-            for par, shift1 in (("e", 0.5), ("o", -0.5)):
-                v = fp.tile([P, 2, C], F32, tag="v" + par, name="v" + par)
-                afn(v[:, 1, :], xf, ACT.Abs, 1.5, shift1)
-                afn(v[:, 0, :], v[:, 1, :], ACT.Abs, 1.0, -2.0)
-                if par == "e":
-                    g = fp.tile([P, C], F32, tag="g", name="g")
-                    afn(g[:], v[:, 0, :], ACT.Abs, 1.0, -1.0)
-                sq = fp.tile([P, C], F32, tag="sq" + par, name="sq" + par)
-                h = fp.tile([P, C], F32, tag="h" + par, name="h" + par)
-                if par == "e":
-                    afn(sq[:], g[:], ACT.Square, -k2, k2 * (1.0 + beta / 2.0))
-                    afn(h[:], g[:], ACT.Identity, 1.0, r0 - 1.0)
-                else:
-                    afn(sq[:], g[:], ACT.Square, k2, k2 * beta / 2.0)
-                    afn(h[:], g[:], ACT.Identity, -1.0, r0)
-                s = fp.tile([P, 2, C], F32, tag="s" + par, name="s" + par)
-                afn(s[:], v[:], ACT.Square, k6, -2.0 * k6)
-                tiles[par] = (v, sq, h, s)
+            v1e = afn("v1e", xf, ACT.Abs, 1.5, 0.5)
+            v1o = afn("v1o", xf, ACT.Abs, 1.5, -0.5)
+            v2e = afn("v2e", v1e[:], ACT.Abs, 1.0, -2.0)
+            v2o = afn("v2o", v1o[:], ACT.Abs, 1.0, -2.0)
+            g = afn("g", v2e[:], ACT.Abs, 1.0, -1.0)
+            s2 = afn("s2", v1e[:], ACT.Square, k6, -2.0 * k6)
+            sqe = afn("sqe", g[:], ACT.Square, -k2, k2 * (1.0 + beta / 2.0))
+            sa = afn("sa", v2e[:], ACT.Square, k6, -2.0 * k6)
+            he = afn("he", g[:], ACT.Identity, 1.0, r0 - 1.0)
+            s3 = afn("s3", v1o[:], ACT.Square, k6, -2.0 * k6)
+            sqo = afn("sqo", g[:], ACT.Square, k2, k2 * beta / 2.0)
+            sb = afn("sb", v2o[:], ACT.Square, k6, -2.0 * k6)
+            ho = afn("ho", g[:], ACT.Identity, -1.0, r0)
+            nc.scalar.activation(out=act[:, 8, :], in_=xf, func=ACT.Silu)
 
-            for par, base, mi in (("e", 0, 0), ("o", 5, 1)):
-                v, sq, h, s = tiles[par]
-                nf = hp.tile([P, C], BF16, tag="nf", name="nf" + par)
-                nc.vector.scalar_tensor_tensor(out=nf[:], in0=sq[:], scalar=dl, in1=h[:], op0=ALU.add, op1=ALU.mult)
-                nw = hp.tile([P, 2, C], BF16, tag="nw", name="nw" + par)
-                nc.vector.scalar_tensor_tensor(
-                    out=nw[:].rearrange("p r w -> p (r w)"),
-                    in0=v[:].rearrange("p r w -> p (r w)"),
-                    scalar=2.0,
-                    in1=s[:].rearrange("p r w -> p (r w)"),
-                    op0=ALU.subtract,
-                    op1=ALU.mult,
-                )
-                if prev is not None:
-                    evacuate(prev, mi)
-                tt(nw[:], nw[:], nf[:].unsqueeze(1).to_broadcast([P, 2, C]), ALU.max)
-                if par == "o":
-                    quantise(1, 5)
-                nc.vector.tensor_scalar(
-                    out=act[:, base : base + 2, :], in0=nw[:], scalar1=0.0, scalar2=-1.0, op0=ALU.min, op1=ALU.mult
-                )
-                mk = below[:, mi, c * C : (c + 1) * C]
-                tt(act[:, base + 2, :], act[:, base, :], mk, ALU.mult)
-                tt(act[:, base + 3, :], act[:, base, :], act[:, base + 2, :], ALU.subtract)
-            quantise(6, 7)
-            quantise(7, 9)
+            nw = hp.tile([P, 2, 2, C], BF16, tag="nw", name="nw%d" % c)
+            nf = hp.tile([P, 2, C], BF16, tag="nf", name="nf%d" % c)
+            stt(nw[:, 1, 0, :], v1e[:], 2.0, s2[:], ALU.subtract)
+            if prev is not None:
+                finish(prev)
+            stt(nw[:, 0, 0, :], v2e[:], 2.0, sa[:], ALU.subtract)
+            stt(nf[:, 0, :], sqe[:], dl, he[:], ALU.add)
+            stt(nw[:, 1, 1, :], v1o[:], 2.0, s3[:], ALU.subtract)
+            stt(nw[:, 0, 1, :], v2o[:], 2.0, sb[:], ALU.subtract)
+            stt(nf[:, 1, :], sqo[:], dl, ho[:], ALU.add)
+            if prev is not None:
+                evacuate(prev, 0)
+            nwv = nw[:].rearrange("p r q w -> p r (q w)")
+            tt(nwv, nwv, nf[:].rearrange("p q w -> p (q w)").unsqueeze(1).to_broadcast([P, 2, 2 * C]), ALU.max)
+            if prev is not None:
+                evacuate(prev, 1)
+            nc.vector.tensor_scalar(
+                out=act[:, 0:4, :].rearrange("p g w -> p (g w)"),
+                in0=nw[:].rearrange("p r q w -> p (r q w)"),
+                scalar1=0.0,
+                scalar2=-1.0,
+                op0=ALU.min,
+                op1=ALU.mult,
+            )
+            quantise(8, 9)
+            tt(act[:, 4:6, :], act[:, 0:2, :], below[:, :, c * C : (c + 1) * C], ALU.mult)
+            quantise(2, 4)
+            tt(act[:, 6:8, :], act[:, 0:2, :], act[:, 4:6, :], ALU.subtract)
 
         def matmuls(c):
-            ac, asc = codes[c]
+            ac, asc, act = codes[c]
             for jj in range(CH_T):
                 acc = pso.tile([P, O], F32, tag="acc", name="acc%d_%d" % (c, jj))
                 accs[(c, jj)] = acc
@@ -240,13 +241,22 @@ def tile_kanoriginal_kernel(tc, x, coef, scale_base_words, scale_base_scales, sc
                 for n, (s, b) in enumerate(PASSES):
                     nc.tensor.matmul_mx(
                         out=acc[:],
-                        lhsT=ac[:, s, cols].bitcast(FP8X4),
-                        lhsT_scale=asc[:, s, cols],
+                        lhsT=ac[:, s - 2, cols].bitcast(FP8X4),
+                        lhsT_scale=asc[:, s - 2, cols],
                         rhs=(w4[:].bitcast(FP4X4) if b < 0 else wc[:, b, :].bitcast(FP8X4)),
                         rhs_scale=(w4s[:] if b < 0 else ws[:, b, :]),
                         start=(n == 0),
                         stop=(n == NB),
                     )
+
+        def finish(c):
+            ac, asc, act = codes[c]
+            nc.vector.quantize_mx(
+                out=ac[:, 2:6, :].rearrange("p g w -> p (g w)").bitcast(FP8X4),
+                scales=asc[:, 2:6, :].rearrange("p g w -> p (g w)"),
+                in_=act[:, 4:8, :].rearrange("p g w -> p (g w)"),
+            )
+            matmuls(c)
 
         transpose_x(0)
         transpose_sp()
@@ -261,12 +271,9 @@ def tile_kanoriginal_kernel(tc, x, coef, scale_base_words, scale_base_scales, sc
         weights(2)
         weights(3)
         quantise_weights()
-        matmuls(0)
         elementwise(1, 0)
-        matmuls(1)
         elementwise(2, 1)
-        matmuls(2)
         elementwise(3, 2)
-        matmuls(3)
+        finish(3)
         evacuate(3, 0)
         evacuate(3, 1)

@@ -22,13 +22,12 @@ NB = 6
 FLOPS = 2 * N_ROWS * D * O * (NB + 1)
 
 TILES = N_ROWS // P
-CH_T = 2
-CHUNKS = TILES // CH_T
-C = CH_T * P * 4
-DVE_COEF = (0,)
+CH = (2, 2, 2, 1, 1)
+W_T = 4 * P
+DVE_COEF = (0, 1)
 MANUAL = True
 N_SLOTS = 9
-PASSES = ((8, -1), (2, 2), (3, 3), (4, 0), (5, 1), (6, 4), (7, 5))
+PASSES = ((4, -1), (1, 2), (2, 0), (3, 4), (6, 3), (7, 1), (8, 5))
 
 
 def tile_kanoriginal_kernel(tc, x, coef, scale_base_words, scale_base_scales, scale_sp, bias, out):
@@ -73,11 +72,11 @@ def tile_kanoriginal_kernel(tc, x, coef, scale_base_words, scale_base_scales, sc
             nc.sync.dma_start(out=ct[:], in_=cv[a])
             coef_sb.append(ct)
 
-        nc.sync.dma_start(out=x_sb[:, 0:2, :], in_=xv[:, 0:2, :])
+        nc.sync.dma_start(out=x_sb[:, 0 : CH[0], :], in_=xv[:, 0 : CH[0], :])
         nc.sync.dma_start(out=sp_sb[:], in_=scale_sp.rearrange("(a o) i -> o a i", o=P))
         load_coef(0)
-        nc.sync.dma_start(out=x_sb[:, 2:8, :], in_=xv[:, 2:8, :])
         load_coef(1)
+        nc.sync.dma_start(out=x_sb[:, CH[0] : TILES, :], in_=xv[:, CH[0] : TILES, :])
         load_coef(2)
         load_coef(3)
         for q in range(4):
@@ -91,15 +90,18 @@ def tile_kanoriginal_kernel(tc, x, coef, scale_base_words, scale_base_scales, sc
         xg = const.tile([P, TILES, P, 4], BF16, align_bytes=64)
         below = const.tile([P, 2, TILES * P * 4], BF16)
 
+        first = [sum(CH[:c]) for c in range(len(CH))]
+
         def transpose_x(c):
+            nt = CH[c]
             xt = pst.tile([P, 512], F32, tag="tp", name="xt%d" % c)
-            xtv = xt[:].rearrange("p (j u n) -> p j u n", j=CH_T, u=2)
-            for jj in range(CH_T):
-                words = x_sb[:, c * CH_T + jj, :].bitcast(F32)
+            xtv = xt[:, 0 : nt * 2 * P].rearrange("p (j u n) -> p j u n", j=nt, u=2)
+            for jj in range(nt):
+                words = x_sb[:, first[c] + jj, :].bitcast(F32)
                 for u in range(2):
                     nc.tensor.transpose(xtv[:, jj, u, :], words[:, u : D // 2 : 2], ident[:])
             nc.vector.tensor_copy(
-                out=xg[:, c * CH_T : (c + 1) * CH_T, :, :].bitcast(F32), in_=xtv.rearrange("p j u n -> p j n u")
+                out=xg[:, first[c] : first[c] + nt, :, :].bitcast(F32), in_=xtv.rearrange("p j u n -> p j n u")
             )
 
         spg = const.tile([P, O, 4], BF16)
@@ -152,42 +154,66 @@ def tile_kanoriginal_kernel(tc, x, coef, scale_base_words, scale_base_scales, sc
                     in_=wg[:, b : b + 2, :, :].rearrange("p b o t -> p (b o t)"),
                 )
 
-        def afn(nm, src, func, scale, shift):
-            t = fp.tile([P, C], F32, tag=nm, name=nm)
-            nc.scalar.activation(out=t[:], in_=src, func=func, scale=scale, bias=shift)
-            return t
-
         def stt(dst, in0, scalar, in1, op0):
             nc.vector.scalar_tensor_tensor(out=dst, in0=in0, scalar=scalar, in1=in1, op0=op0, op1=ALU.mult)
 
         def tt(dst, in0, in1, op_):
             nc.vector.tensor_tensor(out=dst, in0=in0, in1=in1, op=op_)
 
+        def clamp_neg(dst, src):
+            nc.vector.tensor_scalar(out=dst, in0=src, scalar1=0.0, scalar2=-1.0, op0=ALU.min, op1=ALU.mult)
+
         codes = {}
         accs = {}
 
         def evacuate(c, jj):
             if jj == 0:
-                accs[(c, "res")] = op.tile([P, CH_T, O], F32, tag="res", name="res%d" % c)
+                accs[(c, "res")] = op.tile([P, CH[c], O], F32, tag="res", name="res%d" % c)
             res = accs[(c, "res")]
             tt(res[:, jj, :], accs[(c, jj)][:], bias_sb[:], ALU.add)
-            if jj == CH_T - 1:
-                nc.sync.dma_start(out=ov[:, c * CH_T : (c + 1) * CH_T, :], in_=res[:])
+            if jj == CH[c] - 1:
+                nc.sync.dma_start(out=ov[:, first[c] : first[c] + CH[c], :], in_=res[:])
 
-        def elementwise(c, prev):
-            xf = xg[:, c * CH_T : (c + 1) * CH_T, :, :].rearrange("p j n t -> p (j n t)")
-            act = actp.tile([P, N_SLOTS, C], BF16, align_bytes=64, tag="act", name="act%d" % c)
-            ac = qp.tile([P, N_SLOTS - 2, C // 4], U32, align_bytes=64, tag="ac", name="ac%d" % c)
-            asc = qp.tile([P, N_SLOTS - 2, C // 4], U8, align_bytes=64, tag="asc", name="asc%d" % c)
+        def quantise(c, s0, s1):
+            ac, asc, act = codes[c]
+            nc.vector.quantize_mx(
+                out=ac[:, s0:s1, :].rearrange("p g w -> p (g w)").bitcast(FP8X4),
+                scales=asc[:, s0:s1, :].rearrange("p g w -> p (g w)"),
+                in_=act[:, s0:s1, :].rearrange("p g w -> p (g w)"),
+            )
+
+        def matmuls(c):
+            ac, asc, act = codes[c]
+            for jj in range(CH[c]):
+                acc = pso.tile([P, O], F32, tag="acc", name="acc%d_%d" % (c, jj))
+                accs[(c, jj)] = acc
+                cols = slice(jj * P, (jj + 1) * P)
+                for n, (s, b) in enumerate(PASSES):
+                    nc.tensor.matmul_mx(
+                        out=acc[:],
+                        lhsT=ac[:, s, cols].bitcast(FP8X4),
+                        lhsT_scale=asc[:, s, cols],
+                        rhs=(w4[:].bitcast(FP4X4) if b < 0 else wc[:, b, :].bitcast(FP8X4)),
+                        rhs_scale=(w4s[:] if b < 0 else ws[:, b, :]),
+                        start=(n == 0),
+                        stop=(n == NB),
+                    )
+
+        def elementwise(c, prev, last):
+            cw = CH[c] * W_T
+            lo = first[c] * W_T
+            xf = xg[:, first[c] : first[c] + CH[c], :, :].rearrange("p j n t -> p (j n t)")
+            act = actp.tile([P, N_SLOTS, cw], BF16, align_bytes=64, tag="act", name="act%d" % c)
+            ac = qp.tile([P, N_SLOTS, cw // 4], U32, align_bytes=64, tag="ac", name="ac%d" % c)
+            asc = qp.tile([P, N_SLOTS, cw // 4], U8, align_bytes=64, tag="asc", name="asc%d" % c)
             codes[c] = (ac, asc, act)
 
-            def quantise(s0, s1):
-                nc.vector.quantize_mx(
-                    out=ac[:, s0 - 2 : s1 - 2, :].rearrange("p g w -> p (g w)").bitcast(FP8X4),
-                    scales=asc[:, s0 - 2 : s1 - 2, :].rearrange("p g w -> p (g w)"),
-                    in_=act[:, s0:s1, :].rearrange("p g w -> p (g w)"),
-                )
+            def afn(nm, src, func, scale, shift):
+                t = fp.tile([P, cw], F32, tag=nm, name=nm)
+                nc.scalar.activation(out=t[:], in_=src, func=func, scale=scale, bias=shift)
+                return t
 
+            nc.scalar.activation(out=act[:, 4, :], in_=xf, func=ACT.Silu)
             v1e = afn("v1e", xf, ACT.Abs, 1.5, 0.5)
             v1o = afn("v1o", xf, ACT.Abs, 1.5, -0.5)
             v2e = afn("v2e", v1e[:], ACT.Abs, 1.0, -2.0)
@@ -201,79 +227,57 @@ def tile_kanoriginal_kernel(tc, x, coef, scale_base_words, scale_base_scales, sc
             sqo = afn("sqo", g[:], ACT.Square, k2, k2 * beta / 2.0)
             sb = afn("sb", v2o[:], ACT.Square, k6, -2.0 * k6)
             ho = afn("ho", g[:], ACT.Identity, -1.0, r0)
-            nc.scalar.activation(out=act[:, 8, :], in_=xf, func=ACT.Silu)
 
-            nw = hp.tile([P, 2, 2, C], BF16, tag="nw", name="nw%d" % c)
-            nf = hp.tile([P, 2, C], BF16, tag="nf", name="nf%d" % c)
-            stt(nw[:, 1, 0, :], v1e[:], 2.0, s2[:], ALU.subtract)
+            nw = hp.tile([P, 2, 2, cw], BF16, tag="nw", name="nw%d" % c)
+            nf = hp.tile([P, 2, cw], BF16, tag="nf", name="nf%d" % c)
+            actq = [act[:, 5 * q : 5 * q + 4, :] for q in range(2)]
+            low = [below[:, q, lo : lo + cw] for q in range(2)]
+            n_prev = 0 if prev is None else CH[prev]
+
+            def evac_prev(jj):
+                if jj < n_prev:
+                    evacuate(prev, jj)
+
+            stt(nw[:, 0, 1, :], v1e[:], 2.0, s2[:], ALU.subtract)
             if prev is not None:
-                finish(prev)
+                quantise(prev, 7, 9)
+                matmuls(prev)
             stt(nw[:, 0, 0, :], v2e[:], 2.0, sa[:], ALU.subtract)
             stt(nf[:, 0, :], sqe[:], dl, he[:], ALU.add)
             stt(nw[:, 1, 1, :], v1o[:], 2.0, s3[:], ALU.subtract)
-            stt(nw[:, 0, 1, :], v2o[:], 2.0, sb[:], ALU.subtract)
+            tt(nw[:, 0, :, :], nw[:, 0, :, :], nf[:, 0, :].unsqueeze(1).to_broadcast([P, 2, cw]), ALU.max)
+            stt(nw[:, 1, 0, :], v2o[:], 2.0, sb[:], ALU.subtract)
+            clamp_neg(actq[0][:, 0:2, :], nw[:, 0, :, :])
             stt(nf[:, 1, :], sqo[:], dl, ho[:], ALU.add)
-            if prev is not None:
-                evacuate(prev, 0)
-            nwv = nw[:].rearrange("p r q w -> p r (q w)")
-            tt(nwv, nwv, nf[:].rearrange("p q w -> p (q w)").unsqueeze(1).to_broadcast([P, 2, 2 * C]), ALU.max)
-            if prev is not None:
-                evacuate(prev, 1)
-            nc.vector.tensor_scalar(
-                out=act[:, 0:4, :].rearrange("p g w -> p (g w)"),
-                in0=nw[:].rearrange("p r q w -> p (r q w)"),
-                scalar1=0.0,
-                scalar2=-1.0,
-                op0=ALU.min,
-                op1=ALU.mult,
-            )
-            quantise(8, 9)
-            tt(act[:, 4:6, :], act[:, 0:2, :], below[:, :, c * C : (c + 1) * C], ALU.mult)
-            quantise(2, 4)
-            tt(act[:, 6:8, :], act[:, 0:2, :], act[:, 4:6, :], ALU.subtract)
+            evac_prev(0)
+            tt(actq[0][:, 2, :], actq[0][:, 0, :], low[0], ALU.mult)
+            tt(nw[:, 1, :, :], nw[:, 1, :, :], nf[:, 1, :].unsqueeze(1).to_broadcast([P, 2, cw]), ALU.max)
+            tt(actq[0][:, 3, :], actq[0][:, 0, :], actq[0][:, 2, :], ALU.subtract)
+            clamp_neg(actq[1][:, 0:2, :], nw[:, 1, :, :])
+            quantise(c, 1, 5)
+            evac_prev(1)
+            tt(actq[1][:, 2, :], actq[1][:, 0, :], low[1], ALU.mult)
+            quantise(c, 6, 7)
+            tt(actq[1][:, 3, :], actq[1][:, 0, :], actq[1][:, 2, :], ALU.subtract)
+            if last:
+                quantise(c, 7, 9)
+                matmuls(c)
 
-        def matmuls(c):
-            ac, asc, act = codes[c]
-            for jj in range(CH_T):
-                acc = pso.tile([P, O], F32, tag="acc", name="acc%d_%d" % (c, jj))
-                accs[(c, jj)] = acc
-                cols = slice(jj * P, (jj + 1) * P)
-                for n, (s, b) in enumerate(PASSES):
-                    nc.tensor.matmul_mx(
-                        out=acc[:],
-                        lhsT=ac[:, s - 2, cols].bitcast(FP8X4),
-                        lhsT_scale=asc[:, s - 2, cols],
-                        rhs=(w4[:].bitcast(FP4X4) if b < 0 else wc[:, b, :].bitcast(FP8X4)),
-                        rhs_scale=(w4s[:] if b < 0 else ws[:, b, :]),
-                        start=(n == 0),
-                        stop=(n == NB),
-                    )
-
-        def finish(c):
-            ac, asc, act = codes[c]
-            nc.vector.quantize_mx(
-                out=ac[:, 2:6, :].rearrange("p g w -> p (g w)").bitcast(FP8X4),
-                scales=asc[:, 2:6, :].rearrange("p g w -> p (g w)"),
-                in_=act[:, 4:8, :].rearrange("p g w -> p (g w)"),
-            )
-            matmuls(c)
-
+        n_ch = len(CH)
         transpose_x(0)
         transpose_sp()
         weights(0)
-        for c in range(1, CHUNKS):
+        weights(1)
+        for c in range(1, n_ch):
             transpose_x(c)
         xall = xg[:].rearrange("p j n t -> p (j n t)")
         nc.vector.tensor_scalar(out=below[:, 0, :], in0=xall, scalar1=-1.0 / 3.0, scalar2=None, op0=ALU.is_lt)
         nc.vector.tensor_scalar(out=below[:, 1, :], in0=xall, scalar1=1.0 / 3.0, scalar2=None, op0=ALU.is_lt)
-        elementwise(0, None)
-        weights(1)
+        elementwise(0, None, False)
         weights(2)
         weights(3)
         quantise_weights()
-        elementwise(1, 0)
-        elementwise(2, 1)
-        elementwise(3, 2)
-        finish(3)
-        evacuate(3, 0)
-        evacuate(3, 1)
+        for c in range(1, n_ch):
+            elementwise(c, c - 1, c == n_ch - 1)
+        for jj in range(CH[n_ch - 1]):
+            evacuate(n_ch - 1, jj)

@@ -25,7 +25,7 @@ TILES = N_ROWS // P
 CH = (2, 2, 2, 1, 1)
 W_T = 4 * P
 DVE_COEF = (0, 1)
-MANUAL = True
+MANUAL = False
 N_SLOTS = 9
 PASSES = ((4, -1), (1, 2), (2, 0), (3, 4), (6, 3), (7, 1), (8, 5))
 

@@ -27,7 +27,7 @@ W_T = 4 * P
 DVE_COEF = (0, 1)
 MANUAL = False
 N_SLOTS = 9
-PASSES = ((4, -1), (1, 2), (2, 0), (3, 4), (6, 3), (7, 1), (8, 5))
+PASSES = ((8, -1), (2, 2), (3, 3), (4, 0), (5, 1), (6, 4), (7, 5))
 
 
 def tile_kanoriginal_kernel(tc, x, coef, scale_base_words, scale_base_scales, scale_sp, bias, out):
@@ -213,7 +213,7 @@ def tile_kanoriginal_kernel(tc, x, coef, scale_base_words, scale_base_scales, sc
                 nc.scalar.activation(out=t[:], in_=src, func=func, scale=scale, bias=shift)
                 return t
 
-            nc.scalar.activation(out=act[:, 4, :], in_=xf, func=ACT.Silu)
+            nc.scalar.activation(out=act[:, 8, :], in_=xf, func=ACT.Silu)
             v1e = afn("v1e", xf, ACT.Abs, 1.5, 0.5)
             v1o = afn("v1o", xf, ACT.Abs, 1.5, -0.5)
             v2e = afn("v2e", v1e[:], ACT.Abs, 1.0, -2.0)
@@ -230,37 +230,32 @@ def tile_kanoriginal_kernel(tc, x, coef, scale_base_words, scale_base_scales, sc
 
             nw = hp.tile([P, 2, 2, cw], BF16, tag="nw", name="nw%d" % c)
             nf = hp.tile([P, 2, cw], BF16, tag="nf", name="nf%d" % c)
-            actq = [act[:, 5 * q : 5 * q + 4, :] for q in range(2)]
-            low = [below[:, q, lo : lo + cw] for q in range(2)]
             n_prev = 0 if prev is None else CH[prev]
 
             def evac_prev(jj):
                 if jj < n_prev:
                     evacuate(prev, jj)
 
-            stt(nw[:, 0, 1, :], v1e[:], 2.0, s2[:], ALU.subtract)
+            stt(nw[:, 1, 0, :], v1e[:], 2.0, s2[:], ALU.subtract)
             if prev is not None:
-                quantise(prev, 7, 9)
+                quantise(prev, 4, 8)
                 matmuls(prev)
             stt(nw[:, 0, 0, :], v2e[:], 2.0, sa[:], ALU.subtract)
             stt(nf[:, 0, :], sqe[:], dl, he[:], ALU.add)
             stt(nw[:, 1, 1, :], v1o[:], 2.0, s3[:], ALU.subtract)
-            tt(nw[:, 0, :, :], nw[:, 0, :, :], nf[:, 0, :].unsqueeze(1).to_broadcast([P, 2, cw]), ALU.max)
-            stt(nw[:, 1, 0, :], v2o[:], 2.0, sb[:], ALU.subtract)
-            clamp_neg(actq[0][:, 0:2, :], nw[:, 0, :, :])
+            stt(nw[:, 0, 1, :], v2o[:], 2.0, sb[:], ALU.subtract)
             stt(nf[:, 1, :], sqo[:], dl, ho[:], ALU.add)
             evac_prev(0)
-            tt(actq[0][:, 2, :], actq[0][:, 0, :], low[0], ALU.mult)
-            tt(nw[:, 1, :, :], nw[:, 1, :, :], nf[:, 1, :].unsqueeze(1).to_broadcast([P, 2, cw]), ALU.max)
-            tt(actq[0][:, 3, :], actq[0][:, 0, :], actq[0][:, 2, :], ALU.subtract)
-            clamp_neg(actq[1][:, 0:2, :], nw[:, 1, :, :])
-            quantise(c, 1, 5)
+            nwv = nw[:].rearrange("p r q w -> p r (q w)")
+            tt(nwv, nwv, nf[:].rearrange("p q w -> p (q w)").unsqueeze(1).to_broadcast([P, 2, 2 * cw]), ALU.max)
             evac_prev(1)
-            tt(actq[1][:, 2, :], actq[1][:, 0, :], low[1], ALU.mult)
-            quantise(c, 6, 7)
-            tt(actq[1][:, 3, :], actq[1][:, 0, :], actq[1][:, 2, :], ALU.subtract)
+            clamp_neg(act[:, 0:4, :].rearrange("p g w -> p (g w)"), nw[:].rearrange("p r q w -> p (r q w)"))
+            quantise(c, 8, 9)
+            tt(act[:, 4:6, :], act[:, 0:2, :], below[:, :, lo : lo + cw], ALU.mult)
+            quantise(c, 2, 4)
+            tt(act[:, 6:8, :], act[:, 0:2, :], act[:, 4:6, :], ALU.subtract)
             if last:
-                quantise(c, 7, 9)
+                quantise(c, 4, 8)
                 matmuls(c)
 
         n_ch = len(CH)

@@ -24,8 +24,9 @@ FLOPS = 2 * N_ROWS * D * O * (NB + 1)
 TILES = N_ROWS // P
 CH = (2, 2, 2, 1, 1)
 W_T = 4 * P
-DVE_COEF = (0, 1)
-MANUAL = False
+OB = 32
+N_BLK = O // OB
+RUN = 4 * NB * (P - 1) + NB
 N_SLOTS = 9
 PASSES = ((8, -1), (2, 2), (3, 3), (4, 0), (5, 1), (6, 4), (7, 5))
 
@@ -39,16 +40,15 @@ def tile_kanoriginal_kernel(tc, x, coef, scale_base_words, scale_base_scales, sc
     dl = (r0 * beta - beta * beta / 4.0) / 2.0
     with ExitStack() as ctx:
         const = ctx.enter_context(tc.tile_pool(name="const", bufs=1))
-        cpool = ctx.enter_context(tc.tile_pool(name="cpool", bufs=2))
+        cpool = ctx.enter_context(tc.tile_pool(name="cpool", bufs=3))
         fp = ctx.enter_context(tc.tile_pool(name="fp", bufs=1))
         hp = ctx.enter_context(tc.tile_pool(name="hp", bufs=1))
         actp = ctx.enter_context(tc.tile_pool(name="actp", bufs=2))
-        qp = ctx.enter_context(tc.tile_pool(name="qp", bufs=2))
+        qp = ctx.enter_context(tc.tile_pool(name="qp", bufs=1))
         op = ctx.enter_context(tc.tile_pool(name="op", bufs=2))
         pst = ctx.enter_context(tc.psum_pool(name="pst", bufs=4))
         pso = ctx.enter_context(tc.psum_pool(name="pso", bufs=4))
-        if MANUAL:
-            ctx.enter_context(tc.manual_schedule())
+        ctx.enter_context(tc.manual_schedule(engines={mybir.EngineType.DVE}))
 
         w4s = const.tile([P, O], U8, align_bytes=64)
         nc.vector.memset(w4s[:].bitcast(I32), 0)
@@ -56,29 +56,31 @@ def tile_kanoriginal_kernel(tc, x, coef, scale_base_words, scale_base_scales, sc
         nc.vector.memset(warm[:], 0.0)
         ident = const.tile([P, P], F32)
         make_identity(nc, ident[:])
+        ident_bf = const.tile([P, P], BF16)
+        make_identity(nc, ident_bf[:])
         nc.scalar.activation(out=warm[:, 4:8], in_=warm[:, 0:4], func=ACT.Silu)
 
         xv = x.flatten_outer_dims().rearrange("(p j) d -> p j d", j=TILES)
         ov = out.flatten_outer_dims().rearrange("(p j) o -> p j o", j=TILES)
-        cv = coef.rearrange("(a o) i b -> a o (i b)", o=P)
-        x_sb = const.tile([P, TILES, D], BF16)
-        sp_sb = const.tile([P, 4, D], BF16)
+        cflat = coef.rearrange("o i b -> o (i b)")
+        x_sb = [op.tile([P, 4, D], BF16, tag="res", name="x_sb%d" % h) for h in range(2)]
+        sp_sb = hp.tile([P, 4, D], BF16, tag="nf", name="sp_sb")
         w4 = const.tile([P, 2 * O], U8, align_bytes=64)
         bias_sb = const.tile([P, O], BF16)
         coef_sb = []
 
         def load_coef(a):
             ct = cpool.tile([P, D * NB], BF16, tag="coef", name="coef%d" % a)
-            nc.sync.dma_start(out=ct[:], in_=cv[a])
+            for t in range(4):
+                nc.sync.dma_start(out=ct[t:P:4, 0:RUN], in_=cflat[OB * a : OB * (a + 1), NB * t : NB * t + RUN])
             coef_sb.append(ct)
 
-        nc.sync.dma_start(out=x_sb[:, 0 : CH[0], :], in_=xv[:, 0 : CH[0], :])
+        nc.sync.dma_start(out=x_sb[0][:, 0:2, :], in_=xv[:, 0:2, :])
         nc.sync.dma_start(out=sp_sb[:], in_=scale_sp.rearrange("(a o) i -> o a i", o=P))
-        load_coef(0)
-        load_coef(1)
-        nc.sync.dma_start(out=x_sb[:, CH[0] : TILES, :], in_=xv[:, CH[0] : TILES, :])
-        load_coef(2)
-        load_coef(3)
+        nc.sync.dma_start(out=x_sb[0][:, 2:4, :], in_=xv[:, 2:4, :])
+        nc.sync.dma_start(out=x_sb[1][:], in_=xv[:, 4:8, :])
+        for a in range(8):
+            load_coef(a)
         for q in range(4):
             nc.sync.dma_start(
                 out=w4s[32 * q : 32 * q + 4, :].bitcast(I32),
@@ -86,6 +88,8 @@ def tile_kanoriginal_kernel(tc, x, coef, scale_base_words, scale_base_scales, sc
             )
         nc.sync.dma_start(out=w4[:].bitcast(I32), in_=scale_base_words[0].bitcast(I32))
         nc.scalar.dma_start(out=bias_sb[:], in_=bias.partition_broadcast(P))
+        for a in range(8, N_BLK):
+            load_coef(a)
 
         xg = const.tile([P, TILES, P, 4], BF16, align_bytes=64)
         below = const.tile([P, 2, TILES * P * 4], BF16)
@@ -97,7 +101,8 @@ def tile_kanoriginal_kernel(tc, x, coef, scale_base_words, scale_base_scales, sc
             xt = pst.tile([P, 512], F32, tag="tp", name="xt%d" % c)
             xtv = xt[:, 0 : nt * 2 * P].rearrange("p (j u n) -> p j u n", j=nt, u=2)
             for jj in range(nt):
-                words = x_sb[:, first[c] + jj, :].bitcast(F32)
+                j = first[c] + jj
+                words = x_sb[j // 4][:, j % 4, :].bitcast(F32)
                 for u in range(2):
                     nc.tensor.transpose(xtv[:, jj, u, :], words[:, u : D // 2 : 2], ident[:])
             nc.vector.tensor_copy(
@@ -123,36 +128,23 @@ def tile_kanoriginal_kernel(tc, x, coef, scale_base_words, scale_base_scales, sc
                 )
 
         def weights(a):
-            cwords = coef_sb[a][:].bitcast(F32)
+            wt = pst.tile([P, 1024], BF16, tag="tp", name="wt%d" % a)
+            for b in range(NB):
+                nc.tensor.transpose(wt[:, b * P : (b + 1) * P], coef_sb[a][:, b : RUN : 4 * NB], ident_bf[:])
             cols = slice(a * P, (a + 1) * P)
-            for bp in range(3):
-                wt = pst.tile([P, 512], F32, tag="tp", name="wt%d_%d" % (a, bp))
-                for t in range(4):
-                    nc.tensor.transpose(wt[:, t * P : (t + 1) * P], cwords[:, 3 * t + bp : D * 3 : 12], ident[:])
-                src = wt[:].bitcast(BF16).rearrange("p (t o e) -> p e o t", t=4, e=2)
-                dst = wg[:, 2 * bp : 2 * bp + 2, cols, :]
-                if a in DVE_COEF:
-                    nc.vector.tensor_tensor(
-                        out=dst, in0=src, in1=spg[:, cols, :].unsqueeze(1).to_broadcast([P, 2, P, 4]), op=ALU.mult
-                    )
-                else:
-                    nc.scalar.copy(out=dst, in_=src)
-            if a not in DVE_COEF:
-                whole = wg[:, :, cols, :].rearrange("p b o t -> p b (o t)")
-                nc.vector.tensor_tensor(
-                    out=whole,
-                    in0=whole,
-                    in1=spg[:, cols, :].rearrange("p o t -> p (o t)").unsqueeze(1).to_broadcast([P, NB, 4 * P]),
-                    op=ALU.mult,
-                )
+            nc.vector.tensor_tensor(
+                out=wg[:].rearrange("p b o t -> p b (o t)")[:, :, cols],
+                in0=wt[:, 0 : NB * P].rearrange("p (b w) -> p b w", b=NB),
+                in1=spg[:].rearrange("p o t -> p (o t)")[:, cols].unsqueeze(1).to_broadcast([P, NB, P]),
+                op=ALU.mult,
+            )
 
-        def quantise_weights():
-            for b in range(0, NB, 2):
-                nc.vector.quantize_mx(
-                    out=wc[:, b : b + 2, :].rearrange("p b o -> p (b o)").bitcast(FP8X4),
-                    scales=ws[:, b : b + 2, :].rearrange("p b o -> p (b o)"),
-                    in_=wg[:, b : b + 2, :, :].rearrange("p b o t -> p (b o t)"),
-                )
+        def quantise_weights(b):
+            nc.vector.quantize_mx(
+                out=wc[:, b : b + 2, :].rearrange("p b o -> p (b o)").bitcast(FP8X4),
+                scales=ws[:, b : b + 2, :].rearrange("p b o -> p (b o)"),
+                in_=wg[:, b : b + 2, :, :].rearrange("p b o t -> p (b o t)"),
+            )
 
         def stt(dst, in0, scalar, in1, op0):
             nc.vector.scalar_tensor_tensor(out=dst, in0=in0, scalar=scalar, in1=in1, op0=op0, op1=ALU.mult)
@@ -177,8 +169,8 @@ def tile_kanoriginal_kernel(tc, x, coef, scale_base_words, scale_base_scales, sc
         def quantise(c, s0, s1):
             ac, asc, act = codes[c]
             nc.vector.quantize_mx(
-                out=ac[:, s0:s1, :].rearrange("p g w -> p (g w)").bitcast(FP8X4),
-                scales=asc[:, s0:s1, :].rearrange("p g w -> p (g w)"),
+                out=ac[:, s0 - 2 : s1 - 2, :].rearrange("p g w -> p (g w)").bitcast(FP8X4),
+                scales=asc[:, s0 - 2 : s1 - 2, :].rearrange("p g w -> p (g w)"),
                 in_=act[:, s0:s1, :].rearrange("p g w -> p (g w)"),
             )
 
@@ -191,21 +183,21 @@ def tile_kanoriginal_kernel(tc, x, coef, scale_base_words, scale_base_scales, sc
                 for n, (s, b) in enumerate(PASSES):
                     nc.tensor.matmul_mx(
                         out=acc[:],
-                        lhsT=ac[:, s, cols].bitcast(FP8X4),
-                        lhsT_scale=asc[:, s, cols],
+                        lhsT=ac[:, s - 2, cols].bitcast(FP8X4),
+                        lhsT_scale=asc[:, s - 2, cols],
                         rhs=(w4[:].bitcast(FP4X4) if b < 0 else wc[:, b, :].bitcast(FP8X4)),
                         rhs_scale=(w4s[:] if b < 0 else ws[:, b, :]),
                         start=(n == 0),
                         stop=(n == NB),
                     )
 
-        def elementwise(c, prev, last):
+        def elementwise(c, extra):
             cw = CH[c] * W_T
             lo = first[c] * W_T
             xf = xg[:, first[c] : first[c] + CH[c], :, :].rearrange("p j n t -> p (j n t)")
             act = actp.tile([P, N_SLOTS, cw], BF16, align_bytes=64, tag="act", name="act%d" % c)
-            ac = qp.tile([P, N_SLOTS, cw // 4], U32, align_bytes=64, tag="ac", name="ac%d" % c)
-            asc = qp.tile([P, N_SLOTS, cw // 4], U8, align_bytes=64, tag="asc", name="asc%d" % c)
+            ac = qp.tile([P, N_SLOTS - 2, cw // 4], U32, align_bytes=64, tag="ac%d" % c, name="ac%d" % c)
+            asc = qp.tile([P, N_SLOTS - 2, cw // 4], U8, align_bytes=64, tag="asc%d" % c, name="asc%d" % c)
             codes[c] = (ac, asc, act)
 
             def afn(nm, src, func, scale, shift):
@@ -230,49 +222,76 @@ def tile_kanoriginal_kernel(tc, x, coef, scale_base_words, scale_base_scales, sc
 
             nw = hp.tile([P, 2, 2, cw], BF16, tag="nw", name="nw%d" % c)
             nf = hp.tile([P, 2, cw], BF16, tag="nf", name="nf%d" % c)
-            n_prev = 0 if prev is None else CH[prev]
+            nxt = [0]
 
-            def evac_prev(jj):
-                if jj < n_prev:
-                    evacuate(prev, jj)
+            def fill():
+                if nxt[0] < len(extra):
+                    for f in extra[nxt[0]]:
+                        f()
+                    nxt[0] += 1
 
             stt(nw[:, 1, 0, :], v1e[:], 2.0, s2[:], ALU.subtract)
-            if prev is not None:
-                quantise(prev, 4, 8)
-                matmuls(prev)
+            fill()
             stt(nw[:, 0, 0, :], v2e[:], 2.0, sa[:], ALU.subtract)
+            fill()
             stt(nf[:, 0, :], sqe[:], dl, he[:], ALU.add)
+            fill()
             stt(nw[:, 1, 1, :], v1o[:], 2.0, s3[:], ALU.subtract)
+            fill()
             stt(nw[:, 0, 1, :], v2o[:], 2.0, sb[:], ALU.subtract)
+            fill()
             stt(nf[:, 1, :], sqo[:], dl, ho[:], ALU.add)
-            evac_prev(0)
+            fill()
             nwv = nw[:].rearrange("p r q w -> p r (q w)")
             tt(nwv, nwv, nf[:].rearrange("p q w -> p (q w)").unsqueeze(1).to_broadcast([P, 2, 2 * cw]), ALU.max)
-            evac_prev(1)
+            fill()
             clamp_neg(act[:, 0:4, :].rearrange("p g w -> p (g w)"), nw[:].rearrange("p r q w -> p (r q w)"))
+            fill()
             quantise(c, 8, 9)
+            fill()
             tt(act[:, 4:6, :], act[:, 0:2, :], below[:, :, lo : lo + cw], ALU.mult)
+            fill()
             quantise(c, 2, 4)
+            fill()
             tt(act[:, 6:8, :], act[:, 0:2, :], act[:, 4:6, :], ALU.subtract)
-            if last:
-                quantise(c, 4, 8)
-                matmuls(c)
+            for k in range(len(extra)):
+                fill()
 
         n_ch = len(CH)
         transpose_x(0)
         transpose_sp()
-        weights(0)
-        weights(1)
         for c in range(1, n_ch):
             transpose_x(c)
         xall = xg[:].rearrange("p j n t -> p (j n t)")
         nc.vector.tensor_scalar(out=below[:, 0, :], in0=xall, scalar1=-1.0 / 3.0, scalar2=None, op0=ALU.is_lt)
         nc.vector.tensor_scalar(out=below[:, 1, :], in0=xall, scalar1=1.0 / 3.0, scalar2=None, op0=ALU.is_lt)
-        elementwise(0, None, False)
-        weights(2)
-        weights(3)
-        quantise_weights()
-        for c in range(1, n_ch):
-            elementwise(c, c - 1, c == n_ch - 1)
-        for jj in range(CH[n_ch - 1]):
-            evacuate(n_ch - 1, jj)
+        weights(0)
+        weights(1)
+
+        def wgt(a):
+            return [lambda: weights(a)]
+
+        def rest(c):
+            return lambda: quantise(c, 4, 8)
+
+        def mm(c):
+            return lambda: matmuls(c)
+
+        def evac(c, jj):
+            return [lambda: evacuate(c, jj)]
+
+        def qw(b):
+            return lambda: quantise_weights(b)
+
+        idle = []
+        elementwise(0, [wgt(a) for a in range(2, 10)])
+        elementwise(1, [[rest(0)]] + [wgt(a) for a in range(10, N_BLK)])
+        elementwise(
+            2,
+            [[rest(1)], [qw(0)], [qw(2)], [qw(4), mm(0), mm(1)], idle, evac(0, 0), evac(0, 1), idle, evac(1, 0), idle, evac(1, 1)],
+        )
+        elementwise(3, [[rest(2), mm(2)], idle, idle, idle, idle, evac(2, 0), idle, idle, idle, evac(2, 1)])
+        elementwise(4, [[rest(3), mm(3)], idle, idle, idle, idle, evac(3, 0)])
+        quantise(4, 4, 8)
+        matmuls(4)
+        evacuate(4, 0)

@@ -205,20 +205,20 @@ def tile_kanoriginal_kernel(tc, x, coef, scale_base_words, scale_base_scales, sc
                 nc.scalar.activation(out=t[:], in_=src, func=func, scale=scale, bias=shift)
                 return t
 
-            nc.scalar.activation(out=act[:, 8, :], in_=xf, func=ACT.Silu)
             v1e = afn("v1e", xf, ACT.Abs, 1.5, 0.5)
             v1o = afn("v1o", xf, ACT.Abs, 1.5, -0.5)
+            s2 = afn("s2", v1e[:], ACT.Square, k6, -2.0 * k6)
             v2e = afn("v2e", v1e[:], ACT.Abs, 1.0, -2.0)
+            s3 = afn("s3", v1o[:], ACT.Square, k6, -2.0 * k6)
+            sa = afn("sa", v2e[:], ACT.Square, k6, -2.0 * k6)
             v2o = afn("v2o", v1o[:], ACT.Abs, 1.0, -2.0)
             g = afn("g", v2e[:], ACT.Abs, 1.0, -1.0)
-            s2 = afn("s2", v1e[:], ACT.Square, k6, -2.0 * k6)
-            sqe = afn("sqe", g[:], ACT.Square, -k2, k2 * (1.0 + beta / 2.0))
-            sa = afn("sa", v2e[:], ACT.Square, k6, -2.0 * k6)
-            he = afn("he", g[:], ACT.Identity, 1.0, r0 - 1.0)
-            s3 = afn("s3", v1o[:], ACT.Square, k6, -2.0 * k6)
-            sqo = afn("sqo", g[:], ACT.Square, k2, k2 * beta / 2.0)
             sb = afn("sb", v2o[:], ACT.Square, k6, -2.0 * k6)
+            sqe = afn("sqe", g[:], ACT.Square, -k2, k2 * (1.0 + beta / 2.0))
+            he = afn("he", g[:], ACT.Identity, 1.0, r0 - 1.0)
+            sqo = afn("sqo", g[:], ACT.Square, k2, k2 * beta / 2.0)
             ho = afn("ho", g[:], ACT.Identity, -1.0, r0)
+            nc.scalar.activation(out=act[:, 8, :], in_=xf, func=ACT.Silu)
 
             nw = hp.tile([P, 2, 2, cw], BF16, tag="nw", name="nw%d" % c)
             nf = hp.tile([P, 2, cw], BF16, tag="nf", name="nf%d" % c)
@@ -232,13 +232,13 @@ def tile_kanoriginal_kernel(tc, x, coef, scale_base_words, scale_base_scales, sc
 
             stt(nw[:, 1, 0, :], v1e[:], 2.0, s2[:], ALU.subtract)
             fill()
-            stt(nw[:, 0, 0, :], v2e[:], 2.0, sa[:], ALU.subtract)
-            fill()
-            stt(nf[:, 0, :], sqe[:], dl, he[:], ALU.add)
-            fill()
             stt(nw[:, 1, 1, :], v1o[:], 2.0, s3[:], ALU.subtract)
             fill()
+            stt(nw[:, 0, 0, :], v2e[:], 2.0, sa[:], ALU.subtract)
+            fill()
             stt(nw[:, 0, 1, :], v2o[:], 2.0, sb[:], ALU.subtract)
+            fill()
+            stt(nf[:, 0, :], sqe[:], dl, he[:], ALU.add)
             fill()
             stt(nf[:, 1, :], sqo[:], dl, ho[:], ALU.add)
             fill()
@@ -263,10 +263,9 @@ def tile_kanoriginal_kernel(tc, x, coef, scale_base_words, scale_base_scales, sc
         for c in range(1, n_ch):
             transpose_x(c)
         xall = xg[:].rearrange("p j n t -> p (j n t)")
-        nc.vector.tensor_scalar(out=below[:, 0, :], in0=xall, scalar1=-1.0 / 3.0, scalar2=None, op0=ALU.is_lt)
-        nc.vector.tensor_scalar(out=below[:, 1, :], in0=xall, scalar1=1.0 / 3.0, scalar2=None, op0=ALU.is_lt)
-        weights(0)
-        weights(1)
+
+        def mask(q, edge):
+            return [lambda: nc.vector.tensor_scalar(out=below[:, q, :], in0=xall, scalar1=edge, scalar2=None, op0=ALU.is_lt)]
 
         def wgt(a):
             return [lambda: weights(a)]
@@ -284,11 +283,12 @@ def tile_kanoriginal_kernel(tc, x, coef, scale_base_words, scale_base_scales, sc
             return lambda: quantise_weights(b)
 
         idle = []
-        elementwise(0, [wgt(a) for a in range(2, 10)])
-        elementwise(1, [[rest(0)]] + [wgt(a) for a in range(10, N_BLK)])
+        elementwise(0, [mask(0, -1.0 / 3.0), mask(1, 1.0 / 3.0)] + [wgt(a) for a in range(0, 8)])
+        elementwise(1, [[rest(0)]] + [wgt(a) for a in range(8, 14)])
         elementwise(
             2,
-            [[rest(1)], [qw(0)], [qw(2)], [qw(4), mm(0), mm(1)], idle, evac(0, 0), evac(0, 1), idle, evac(1, 0), idle, evac(1, 1)],
+            [[rest(1)], wgt(14), wgt(15), [qw(0)], [qw(2)], [qw(4), mm(0), mm(1)], evac(0, 0), evac(0, 1), idle, evac(1, 0), idle]
+            + [evac(1, 1)],
         )
         elementwise(3, [[rest(2), mm(2)], idle, idle, idle, idle, evac(2, 0), idle, idle, idle, evac(2, 1)])
         elementwise(4, [[rest(3), mm(3)], idle, idle, idle, idle, evac(3, 0)])

@@ -290,8 +290,8 @@ def tile_kanoriginal_kernel(tc, x, coef, scale_base_words, scale_base_scales, sc
             [[rest(1)], wgt(14), wgt(15), [qw(0)], [qw(2)], [qw(4), mm(0), mm(1)], evac(0, 0), evac(0, 1), idle, evac(1, 0), idle]
             + [evac(1, 1)],
         )
-        elementwise(3, [[rest(2), mm(2)], idle, idle, idle, idle, evac(2, 0), idle, idle, idle, evac(2, 1)])
-        elementwise(4, [[rest(3), mm(3)], idle, idle, idle, idle, evac(3, 0)])
-        quantise(4, 4, 8)
+        elementwise(3, [[rest(2), mm(2)], idle, idle, idle, idle, evac(2, 0), evac(2, 1)])
+        elementwise(4, [[rest(3), mm(3)], idle, idle, idle, idle, evac(3, 0), idle, idle, idle, idle, [lambda: quantise(4, 4, 6)]])
+        quantise(4, 6, 8)
         matmuls(4)
         evacuate(4, 0)

@@ -177,7 +177,10 @@ def tile_kanoriginal_kernel(tc, x, coef, scale_base_words, scale_base_scales, sc
         def matmuls(c):
             ac, asc, act = codes[c]
             for jj in range(CH[c]):
-                acc = pso.tile([P, O], F32, tag="acc", name="acc%d_%d" % (c, jj))
+                if c < 2:
+                    acc = pso.tile([P, O], F32, tag="acc", name="acc%d_%d" % (c, jj))
+                else:
+                    acc = pst.tile([P, O], F32, tag="tp", name="acc%d_%d" % (c, jj))
                 accs[(c, jj)] = acc
                 cols = slice(jj * P, (jj + 1) * P)
                 for n, (s, b) in enumerate(PASSES):
@@ -287,11 +290,13 @@ def tile_kanoriginal_kernel(tc, x, coef, scale_base_words, scale_base_scales, sc
         elementwise(1, [[rest(0)]] + [wgt(a) for a in range(8, 14)])
         elementwise(
             2,
-            [[rest(1)], wgt(14), wgt(15), [qw(0)], [qw(2)], [qw(4), mm(0), mm(1)], evac(0, 0), evac(0, 1), idle, evac(1, 0), idle]
-            + [evac(1, 1)],
+            [[rest(1)], idle, wgt(14), wgt(15), [qw(0)], [qw(2)], [qw(4), mm(0), mm(1)], idle, idle, idle, idle, evac(0, 0)],
         )
-        elementwise(3, [[rest(2), mm(2)], idle, idle, idle, idle, evac(2, 0), evac(2, 1)])
-        elementwise(4, [[rest(3), mm(3)], idle, idle, idle, idle, evac(3, 0), idle, idle, idle, idle, [lambda: quantise(4, 4, 6)]])
+        elementwise(3, [[rest(2), mm(2)], evac(0, 1), idle, evac(1, 0), idle, evac(1, 1), evac(2, 0)])
+        elementwise(
+            4, [[rest(3), mm(3)], idle, idle, idle, idle, evac(2, 1), idle, idle, idle, idle, [lambda: quantise(4, 4, 6)]]
+        )
         quantise(4, 6, 8)
         matmuls(4)
+        evacuate(3, 0)
         evacuate(4, 0)

@@ -48,7 +48,7 @@ def tile_kanoriginal_kernel(tc, x, coef, scale_base_words, scale_base_scales, sc
         op = ctx.enter_context(tc.tile_pool(name="op", bufs=2))
         pst = ctx.enter_context(tc.psum_pool(name="pst", bufs=4))
         pso = ctx.enter_context(tc.psum_pool(name="pso", bufs=4))
-        ctx.enter_context(tc.manual_schedule(engines={mybir.EngineType.DVE}))
+        ctx.enter_context(tc.manual_schedule(engines={mybir.EngineType.DVE, mybir.EngineType.SP}))
 
         w4s = const.tile([P, O], U8, align_bytes=64)
         nc.vector.memset(w4s[:].bitcast(I32), 0)
@@ -87,7 +87,7 @@ def tile_kanoriginal_kernel(tc, x, coef, scale_base_words, scale_base_scales, sc
                 in_=scale_base_scales[0, 4 * q : 4 * q + 4, :].bitcast(I32),
             )
         nc.sync.dma_start(out=w4[:].bitcast(I32), in_=scale_base_words[0].bitcast(I32))
-        nc.scalar.dma_start(out=bias_sb[:], in_=bias.partition_broadcast(P))
+        nc.sync.dma_start(out=bias_sb[:], in_=bias.partition_broadcast(P))
         for a in range(8, N_BLK):
             load_coef(a)
 

@@ -79,7 +79,7 @@ def tile_kanoriginal_kernel(tc, x, coef, scale_base_words, scale_base_scales, sc
         nc.sync.dma_start(out=sp_sb[:], in_=scale_sp.rearrange("(a o) i -> o a i", o=P))
         nc.sync.dma_start(out=x_sb[0][:, 2:4, :], in_=xv[:, 2:4, :])
         nc.sync.dma_start(out=x_sb[1][:], in_=xv[:, 4:8, :])
-        for a in range(8):
+        for a in range(N_BLK):
             load_coef(a)
         for q in range(4):
             nc.sync.dma_start(
@@ -88,8 +88,6 @@ def tile_kanoriginal_kernel(tc, x, coef, scale_base_words, scale_base_scales, sc
             )
         nc.sync.dma_start(out=w4[:].bitcast(I32), in_=scale_base_words[0].bitcast(I32))
         nc.sync.dma_start(out=bias_sb[:], in_=bias.partition_broadcast(P))
-        for a in range(8, N_BLK):
-            load_coef(a)
 
         xg = const.tile([P, TILES, P, 4], BF16, align_bytes=64)
         below = const.tile([P, 2, TILES * P * 4], BF16)

@@ -297,4 +297,8 @@ def tile_kanoriginal_kernel(tc, x, coef, scale_base_words, scale_base_scales, sc
         quantise(4, 6, 8)
         matmuls(4)
         evacuate(3, 0)
-        evacuate(4, 0)
+        last = op.tile([P, O], F32, tag="res", name="res_last")
+        for hf in range(2):
+            cols = slice(hf * (O // 2), (hf + 1) * (O // 2))
+            tt(last[:, cols], accs[(4, 0)][:, cols], bias_sb[:, cols], ALU.add)
+            nc.sync.dma_start(out=ov[:, TILES - 1, cols], in_=last[:, cols])

@@ -59,6 +59,11 @@ def tile_kanoriginal_kernel(tc, x, coef, scale_base_words, scale_base_scales, sc
         ident_bf = const.tile([P, P], BF16)
         make_identity(nc, ident_bf[:])
         nc.scalar.activation(out=warm[:, 4:8], in_=warm[:, 0:4], func=ACT.Silu)
+        zeros = const.tile([P, 512], BF16)
+        nc.vector.memset(zeros[:], 0.0)
+        spin = pso.tile([P, 512], F32, tag="acc", name="spin")
+        for k in range(3):
+            nc.tensor.matmul(out=spin[:], lhsT=zeros[:, 0:P], rhs=zeros[:], start=True, stop=True)
 
         xv = x.flatten_outer_dims().rearrange("(p j) d -> p j d", j=TILES)
         ov = out.flatten_outer_dims().rearrange("(p j) o -> p j o", j=TILES)

@@ -297,7 +297,7 @@ def tile_kanoriginal_kernel(tc, x, coef, scale_base_words, scale_base_scales, sc
         )
         elementwise(3, [[rest(2), mm(2)], evac(0, 1), idle, evac(1, 0), idle, evac(1, 1), evac(2, 0)])
         elementwise(
-            4, [[rest(3), mm(3)], idle, idle, idle, idle, evac(2, 1), idle, idle, idle, idle, [lambda: quantise(4, 4, 6)]]
+            4, [idle, idle, idle, idle, idle, [rest(3), mm(3)], evac(2, 1), idle, idle, idle, [lambda: quantise(4, 4, 6)]]
         )
         quantise(4, 6, 8)
         matmuls(4)

import math
from contextlib import ExitStack

import concourse.mybir as mybir
from concourse.masks import make_identity

F32 = mybir.dt.float32
BF16 = mybir.dt.bfloat16
U8 = mybir.dt.uint8
U32 = mybir.dt.uint32
I32 = mybir.dt.int32
FP8X4 = mybir.dt.float8_e4m3fn_x4
FP4X4 = mybir.dt.float4_e2m1fn_x4
ALU = mybir.AluOpType
ACT = mybir.ActivationFunctionType

P = 128
N_ROWS = 1024
D = 512
O = 512
NB = 6
FLOPS = 2 * N_ROWS * D * O * (NB + 1)

TILES = N_ROWS // P
CH = (2, 2, 2, 1, 1)
W_T = 4 * P
OB = 32
N_BLK = O // OB
RUN = 4 * NB * (P - 1) + NB
N_SLOTS = 9
PASSES = ((8, -1), (2, 2), (3, 3), (4, 0), (5, 1), (6, 4), (7, 5))


def tile_kanoriginal_kernel(tc, x, coef, scale_base_words, scale_base_scales, scale_sp, bias, out):
    nc = tc.nc
    k6 = math.sqrt(1.0 / 6.0)
    k2 = math.sqrt(0.5)
    r0 = (2.0 - 2.0 ** (2.0 / 3.0) - 2.0 ** (4.0 / 3.0)) / 3.0
    beta = r0 - 2.0
    dl = (r0 * beta - beta * beta / 4.0) / 2.0
    with ExitStack() as ctx:
        const = ctx.enter_context(tc.tile_pool(name="const", bufs=1))
        cpool = ctx.enter_context(tc.tile_pool(name="cpool", bufs=3))
        fp = ctx.enter_context(tc.tile_pool(name="fp", bufs=1))
        hp = ctx.enter_context(tc.tile_pool(name="hp", bufs=1))
        actp = ctx.enter_context(tc.tile_pool(name="actp", bufs=2))
        qp = ctx.enter_context(tc.tile_pool(name="qp", bufs=1))
        op = ctx.enter_context(tc.tile_pool(name="op", bufs=2))
        pst = ctx.enter_context(tc.psum_pool(name="pst", bufs=4))
        pso = ctx.enter_context(tc.psum_pool(name="pso", bufs=4))
        ctx.enter_context(tc.manual_schedule(engines={mybir.EngineType.DVE, mybir.EngineType.SP}))

        w4s = const.tile([P, O], U8, align_bytes=64)
        nc.vector.memset(w4s[:].bitcast(I32), 0)
        warm = const.tile([P, 8], F32)
        nc.vector.memset(warm[:], 0.0)
        ident = const.tile([P, P], F32)
        make_identity(nc, ident[:])
        ident_bf = const.tile([P, P], BF16)
        make_identity(nc, ident_bf[:])
        nc.scalar.activation(out=warm[:, 4:8], in_=warm[:, 0:4], func=ACT.Silu)
        zeros = const.tile([P, 512], BF16)
        nc.vector.memset(zeros[:], 0.0)
        spin = pso.tile([P, 512], F32, tag="acc", name="spin")
        for k in range(3):
            nc.tensor.matmul(out=spin[:], lhsT=zeros[:, 0:P], rhs=zeros[:], start=True, stop=True)

        xv = x.flatten_outer_dims().rearrange("(p j) d -> p j d", j=TILES)
        ov = out.flatten_outer_dims().rearrange("(p j) o -> p j o", j=TILES)
        cflat = coef.rearrange("o i b -> o (i b)")
        x_sb = [op.tile([P, 4, D], BF16, tag="res", name="x_sb%d" % h) for h in range(2)]
        sp_sb = hp.tile([P, 4, D], BF16, tag="nf", name="sp_sb")
        w4 = const.tile([P, 2 * O], U8, align_bytes=64)
        bias_sb = const.tile([P, O], BF16)
        coef_sb = []

        def load_coef(a):
            ct = cpool.tile([P, D * NB], BF16, tag="coef", name="coef%d" % a)
            for t in range(4):
                nc.sync.dma_start(out=ct[t:P:4, 0:RUN], in_=cflat[OB * a : OB * (a + 1), NB * t : NB * t + RUN])
            coef_sb.append(ct)

        nc.sync.dma_start(out=x_sb[0][:, 0:2, :], in_=xv[:, 0:2, :])
        nc.sync.dma_start(out=sp_sb[:], in_=scale_sp.rearrange("(a o) i -> o a i", o=P))
        nc.sync.dma_start(out=x_sb[0][:, 2:4, :], in_=xv[:, 2:4, :])
        nc.sync.dma_start(out=x_sb[1][:], in_=xv[:, 4:8, :])
        for a in range(N_BLK):
            load_coef(a)
        for q in range(4):
            nc.sync.dma_start(
                out=w4s[32 * q : 32 * q + 4, :].bitcast(I32),
                in_=scale_base_scales[0, 4 * q : 4 * q + 4, :].bitcast(I32),
            )
        nc.sync.dma_start(out=w4[:].bitcast(I32), in_=scale_base_words[0].bitcast(I32))
        nc.sync.dma_start(out=bias_sb[:], in_=bias.partition_broadcast(P))

        xg = const.tile([P, TILES, P, 4], BF16, align_bytes=64)
        below = const.tile([P, 2, TILES * P * 4], BF16)

        first = [sum(CH[:c]) for c in range(len(CH))]

        def transpose_x(c):
            nt = CH[c]
            xt = pst.tile([P, 512], F32, tag="tp", name="xt%d" % c)
            xtv = xt[:, 0 : nt * 2 * P].rearrange("p (j u n) -> p j u n", j=nt, u=2)
            for jj in range(nt):
                j = first[c] + jj
                words = x_sb[j // 4][:, j % 4, :].bitcast(F32)
                for u in range(2):
                    nc.tensor.transpose(xtv[:, jj, u, :], words[:, u : D // 2 : 2], ident[:])
            nc.vector.tensor_copy(
                out=xg[:, first[c] : first[c] + nt, :, :].bitcast(F32), in_=xtv.rearrange("p j u n -> p j n u")
            )

        spg = const.tile([P, O, 4], BF16)
        wg = const.tile([P, NB, O, 4], BF16, align_bytes=64)
        wc = const.tile([P, NB, O], U32, align_bytes=64)
        ws = const.tile([P, NB, O], U8, align_bytes=64)

        def transpose_sp():
            for h in range(2):
                st = pst.tile([P, 512], F32, tag="tp", name="st%d" % h)
                stv = st[:].rearrange("p (a u o) -> p a u o", a=2, u=2)
                for aa in range(2):
                    words = sp_sb[:, 2 * h + aa, :].bitcast(F32)
                    for u in range(2):
                        nc.tensor.transpose(stv[:, aa, u, :], words[:, u : D // 2 : 2], ident[:])
                nc.vector.tensor_copy(
                    out=spg[:, 256 * h : 256 * (h + 1), :].bitcast(F32).rearrange("p (a o) u -> p a o u", a=2),
                    in_=stv.rearrange("p a u o -> p a o u"),
                )

        def weights(a):
            wt = pst.tile([P, 1024], BF16, tag="tp", name="wt%d" % a)
            for b in range(NB):
                nc.tensor.transpose(wt[:, b * P : (b + 1) * P], coef_sb[a][:, b : RUN : 4 * NB], ident_bf[:])
            cols = slice(a * P, (a + 1) * P)
            nc.vector.tensor_tensor(
                out=wg[:].rearrange("p b o t -> p b (o t)")[:, :, cols],
                in0=wt[:, 0 : NB * P].rearrange("p (b w) -> p b w", b=NB),
                in1=spg[:].rearrange("p o t -> p (o t)")[:, cols].unsqueeze(1).to_broadcast([P, NB, P]),
                op=ALU.mult,
            )

        def quantise_weights(b):
            nc.vector.quantize_mx(
                out=wc[:, b : b + 2, :].rearrange("p b o -> p (b o)").bitcast(FP8X4),
                scales=ws[:, b : b + 2, :].rearrange("p b o -> p (b o)"),
                in_=wg[:, b : b + 2, :, :].rearrange("p b o t -> p (b o t)"),
            )

        def stt(dst, in0, scalar, in1, op0):
            nc.vector.scalar_tensor_tensor(out=dst, in0=in0, scalar=scalar, in1=in1, op0=op0, op1=ALU.mult)

        def tt(dst, in0, in1, op_):
            nc.vector.tensor_tensor(out=dst, in0=in0, in1=in1, op=op_)

        def clamp_neg(dst, src):
            nc.vector.tensor_scalar(out=dst, in0=src, scalar1=0.0, scalar2=-1.0, op0=ALU.min, op1=ALU.mult)

        codes = {}
        accs = {}

        def evacuate(c, jj):
            if jj == 0:
                accs[(c, "res")] = op.tile([P, CH[c], O], F32, tag="res", name="res%d" % c)
            res = accs[(c, "res")]
            tt(res[:, jj, :], accs[(c, jj)][:], bias_sb[:], ALU.add)
            if jj == CH[c] - 1:
                nc.sync.dma_start(out=ov[:, first[c] : first[c] + CH[c], :], in_=res[:])

        def quantise(c, s0, s1):
            ac, asc, act = codes[c]
            nc.vector.quantize_mx(
                out=ac[:, s0 - 2 : s1 - 2, :].rearrange("p g w -> p (g w)").bitcast(FP8X4),
                scales=asc[:, s0 - 2 : s1 - 2, :].rearrange("p g w -> p (g w)"),
                in_=act[:, s0:s1, :].rearrange("p g w -> p (g w)"),
            )

        def matmuls(c):
            ac, asc, act = codes[c]
            for jj in range(CH[c]):
                if c < 2:
                    acc = pso.tile([P, O], F32, tag="acc", name="acc%d_%d" % (c, jj))
                else:
                    acc = pst.tile([P, O], F32, tag="tp", name="acc%d_%d" % (c, jj))
                accs[(c, jj)] = acc
                cols = slice(jj * P, (jj + 1) * P)
                for n, (s, b) in enumerate(PASSES):
                    nc.tensor.matmul_mx(
                        out=acc[:],
                        lhsT=ac[:, s - 2, cols].bitcast(FP8X4),
                        lhsT_scale=asc[:, s - 2, cols],
                        rhs=(w4[:].bitcast(FP4X4) if b < 0 else wc[:, b, :].bitcast(FP8X4)),
                        rhs_scale=(w4s[:] if b < 0 else ws[:, b, :]),
                        start=(n == 0),
                        stop=(n == NB),
                    )

        def elementwise(c, extra):
            cw = CH[c] * W_T
            lo = first[c] * W_T
            xf = xg[:, first[c] : first[c] + CH[c], :, :].rearrange("p j n t -> p (j n t)")
            act = actp.tile([P, N_SLOTS, cw], BF16, align_bytes=64, tag="act", name="act%d" % c)
            ac = qp.tile([P, N_SLOTS - 2, cw // 4], U32, align_bytes=64, tag="ac%d" % c, name="ac%d" % c)
            asc = qp.tile([P, N_SLOTS - 2, cw // 4], U8, align_bytes=64, tag="asc%d" % c, name="asc%d" % c)
            codes[c] = (ac, asc, act)

            def afn(nm, src, func, scale, shift):
                t = fp.tile([P, cw], F32, tag=nm, name=nm)
                nc.scalar.activation(out=t[:], in_=src, func=func, scale=scale, bias=shift)
                return t

            v1e = afn("v1e", xf, ACT.Abs, 1.5, 0.5)
            v1o = afn("v1o", xf, ACT.Abs, 1.5, -0.5)
            s2 = afn("s2", v1e[:], ACT.Square, k6, -2.0 * k6)
            v2e = afn("v2e", v1e[:], ACT.Abs, 1.0, -2.0)
            s3 = afn("s3", v1o[:], ACT.Square, k6, -2.0 * k6)
            sa = afn("sa", v2e[:], ACT.Square, k6, -2.0 * k6)
            v2o = afn("v2o", v1o[:], ACT.Abs, 1.0, -2.0)
            g = afn("g", v2e[:], ACT.Abs, 1.0, -1.0)
            sb = afn("sb", v2o[:], ACT.Square, k6, -2.0 * k6)
            sqe = afn("sqe", g[:], ACT.Square, -k2, k2 * (1.0 + beta / 2.0))
            he = afn("he", g[:], ACT.Identity, 1.0, r0 - 1.0)
            sqo = afn("sqo", g[:], ACT.Square, k2, k2 * beta / 2.0)
            ho = afn("ho", g[:], ACT.Identity, -1.0, r0)
            nc.scalar.activation(out=act[:, 8, :], in_=xf, func=ACT.Silu)

            nw = hp.tile([P, 2, 2, cw], BF16, tag="nw", name="nw%d" % c)
            nf = hp.tile([P, 2, cw], BF16, tag="nf", name="nf%d" % c)
            nxt = [0]

            def fill():
                if nxt[0] < len(extra):
                    for f in extra[nxt[0]]:
                        f()
                    nxt[0] += 1

            stt(nw[:, 1, 0, :], v1e[:], 2.0, s2[:], ALU.subtract)
            fill()
            stt(nw[:, 1, 1, :], v1o[:], 2.0, s3[:], ALU.subtract)
            fill()
            stt(nw[:, 0, 0, :], v2e[:], 2.0, sa[:], ALU.subtract)
            fill()
            stt(nw[:, 0, 1, :], v2o[:], 2.0, sb[:], ALU.subtract)
            fill()
            stt(nf[:, 0, :], sqe[:], dl, he[:], ALU.add)
            fill()
            stt(nf[:, 1, :], sqo[:], dl, ho[:], ALU.add)
            fill()
            nwv = nw[:].rearrange("p r q w -> p r (q w)")
            tt(nwv, nwv, nf[:].rearrange("p q w -> p (q w)").unsqueeze(1).to_broadcast([P, 2, 2 * cw]), ALU.max)
            fill()
            clamp_neg(act[:, 0:4, :].rearrange("p g w -> p (g w)"), nw[:].rearrange("p r q w -> p (r q w)"))
            fill()
            quantise(c, 8, 9)
            fill()
            tt(act[:, 4:6, :], act[:, 0:2, :], below[:, :, lo : lo + cw], ALU.mult)
            fill()
            quantise(c, 2, 4)
            fill()
            tt(act[:, 6:8, :], act[:, 0:2, :], act[:, 4:6, :], ALU.subtract)
            for k in range(len(extra)):
                fill()

        n_ch = len(CH)
        transpose_x(0)
        transpose_sp()
        for c in range(1, n_ch):
            transpose_x(c)
        xall = xg[:].rearrange("p j n t -> p (j n t)")

        def mask(q, edge):
            return [lambda: nc.vector.tensor_scalar(out=below[:, q, :], in0=xall, scalar1=edge, scalar2=None, op0=ALU.is_lt)]

        def wgt(a):
            return [lambda: weights(a)]

        def rest(c):
            return lambda: quantise(c, 4, 8)

        def mm(c):
            return lambda: matmuls(c)

        def evac(c, jj):
            return [lambda: evacuate(c, jj)]

        def qw(b):
            return lambda: quantise_weights(b)

        idle = []
        elementwise(0, [mask(0, -1.0 / 3.0), mask(1, 1.0 / 3.0)] + [wgt(a) for a in range(0, 8)])
        elementwise(1, [[rest(0)]] + [wgt(a) for a in range(8, 14)])
        elementwise(
            2,
            [[rest(1)], idle, wgt(14), wgt(15), [qw(0)], [qw(2)], [qw(4), mm(0), mm(1)], idle, idle, idle, idle, evac(0, 0)],
        )
        elementwise(3, [[rest(2), mm(2)], evac(0, 1), idle, evac(1, 0), idle, evac(1, 1), evac(2, 0)])
        elementwise(
            4, [idle, idle, idle, idle, idle, [rest(3), mm(3)], evac(2, 1), idle, idle, idle, [lambda: quantise(4, 4, 6)]]
        )
        quantise(4, 6, 8)
        matmuls(4)
        evacuate(3, 0)
        last = op.tile([P, O], F32, tag="res", name="res_last")
        for hf in range(2):
            cols = slice(hf * (O // 2), (hf + 1) * (O // 2))
            tt(last[:, cols], accs[(4, 0)][:, cols], bias_sb[:, cols], ALU.add)
            nc.sync.dma_start(out=ov[:, TILES - 1, cols], in_=last[:, cols])
